import numpy as np
import ml_dtypes


def mxq(x, axis, fmt="e4m3"):
    dtype, down = {"e4m3": (ml_dtypes.float8_e4m3fn, 7), "e5m2": (ml_dtypes.float8_e5m2, 14)}[fmt]
    v = np.moveaxis(np.asarray(x, np.float32).astype(ml_dtypes.bfloat16).astype(np.float64), axis, -1)
    blocks = v.reshape(v.shape[:-1] + (-1, 32))
    amax = np.abs(blocks).max(-1, keepdims=True)
    byte = np.maximum(np.where(amax > 0, np.frexp(amax)[1] - 1 + 127, 0) - down, 1)
    scale = np.exp2(byte - 127.0)
    codes = (blocks / scale).astype(np.float32).astype(dtype).astype(np.float64)
    return np.moveaxis((codes * scale).reshape(v.shape), -1, axis)


WIDE = False


def mx_kscale(k):
    if not WIDE:
        return np.ones(k)
    levels = np.array([10, -10, 5, -5, 0])
    if k % 512:
        return np.exp2(np.random.permutation(np.resize(levels, k // 32))).repeat(32)
    a = np.empty((k // 512, 16))
    for p in range(k // 512):
        a[p, :8] = np.random.permutation(np.resize(levels, 8))
        for g in range(8):
            far = levels[np.abs(levels - a[p, g]) >= 10]
            a[p, g + 8] = far[np.random.randint(len(far))]
    return np.exp2(a.ravel()).repeat(32)


BF16 = ml_dtypes.bfloat16


def bf(x):
    return np.asarray(x, np.float32).astype(BF16)


def f64(x):
    return np.asarray(x).astype(np.float64)


B, J, C, K, H = 8, 128, 512, 4, 256
KJ = K * J
EPS = 1e-5


def layernorm(v, g, b):
    m = v.mean(-1, keepdims=True)
    var = v.var(-1, keepdims=True)
    return (v - m) / np.sqrt(var + EPS) * g + b


def gcn(xin, adj, spatial_adj, conv_w, conv_b, s_ctx):
    h = (mxq(xin, 2, "e4m3") @ mxq(conv_w, 1, "e4m3").T) + conv_b
    h = h.reshape(B, J, K, C).transpose(0, 2, 1, 3).reshape(B, KJ, C)
    sadj = np.broadcast_to(spatial_adj[None], (B, K - 1, J, J))
    adj4 = np.concatenate([adj * s_ctx, sadj], axis=1).reshape(B, KJ, J)
    return mxq(adj4, 1, "e4m3").transpose(0, 2, 1) @ mxq(h, 1, "e4m3")


def setup_inputs():
    s = mx_kscale(C)
    t = np.sort(mx_kscale(KJ))[np.arange(K) * (KJ - 1) // (K - 1)]
    tw = np.repeat(t, C)
    a = 2.0 / np.sqrt(KJ)
    return {"g1": bf(np.random.standard_normal((B, J, C)) * 0.9 * s),
            "res1": bf(np.random.standard_normal((B, J, C))),
            "adj": bf(np.random.random((B, 1, J, J)) * a / t[0]),
            "spatial_adj": bf(np.random.random((K - 1, J, J)) * a / t[1:, None, None]),
            "conv2_w": bf(np.random.standard_normal((K * C, C)) / np.sqrt(C) / s[None, :] * tw[:, None]),
            "conv2_b": bf(np.random.standard_normal(K * C) * 0.05 * tw),
            "s2": bf(1.5 + 0.1 * np.random.standard_normal(1)),
            "norm2_g": bf(1.0 + 0.1 * np.random.standard_normal(C)),
            "norm2_b": bf(0.1 * np.random.standard_normal(C))}


def reference(g1, res1, adj, spatial_adj, conv2_w, conv2_b, s2, norm2_g, norm2_b):
    g2 = gcn(f64(g1), f64(adj), f64(spatial_adj), f64(conv2_w), f64(conv2_b), f64(s2))
    x2 = f64(res1) + g2
    xn = layernorm(x2, f64(norm2_g), f64(norm2_b))
    return x2, xn

@@ -1,0 +1,296 @@
+from contextlib import ExitStack
+
+import concourse.mybir as mybir
+from concourse.masks import make_identity
+
+F32 = mybir.dt.float32
+BF16 = mybir.dt.bfloat16
+U32 = mybir.dt.uint32
+U8 = mybir.dt.uint8
+FP8X4 = mybir.dt.float8_e4m3fn_x4
+ACT = mybir.ActivationFunctionType
+ALU = mybir.AluOpType
+
+P = 128
+PACK = 4
+B = 8
+J = 128
+C = 512
+K = 4
+R = J // PACK
+CHUNKS = C // P
+GROUP = 4
+N_GROUPS = B // GROUP
+EPS = 1e-5
+
+FLOPS = 2 * B * J * C * K * C + 2 * B * J * K * J * C
+
+
+def tile_block_attention_guide_pb_kernel(
+    tc, g1, res1, adj, spatial_adj, conv2_w, conv2_b, s2, norm2_g, norm2_b, out_0, out_1
+):
+    nc = tc.nc
+    with ExitStack() as ctx:
+        ctx.enter_context(tc.manual_schedule())
+        keep = ctx.enter_context(tc.tile_pool(name="keep", bufs=1))
+        per_group = ctx.enter_context(tc.tile_pool(name="per_group", bufs=2))
+        per_sample = ctx.enter_context(tc.tile_pool(name="per_sample", bufs=3))
+        psum_tr = ctx.enter_context(tc.psum_pool(name="psum_tr", bufs=4))
+        psum_s1 = ctx.enter_context(tc.psum_pool(name="psum_s1", bufs=3))
+        psum_s2 = ctx.enter_context(tc.psum_pool(name="psum_s2", bufs=1))
+
+        g1_sb = keep.tile([P, B, C], BF16)
+        w_sb = keep.tile([P, CHUNKS, K, C], BF16)
+        res1_sb = keep.tile([P, B, C], BF16)
+        w_by_chunk = conv2_w.rearrange("(k q p) c -> q p k c", k=K, q=CHUNKS)
+        nc.sync.dma_start(out=g1_sb[:, 0:GROUP], in_=g1[0:GROUP].rearrange("b j c -> j b c"))
+        nc.sync.dma_start(out=w_sb[:, 0], in_=w_by_chunk[0])
+        bias_rows = keep.tile([P, P], BF16)
+        nc.vector.memset(bias_rows[:], 0.0)
+        nc.sync.dma_start(out=bias_rows[0 : K * CHUNKS, :], in_=conv2_b.rearrange("(i p) -> i p", p=P))
+        for q in range(1, CHUNKS):
+            nc.sync.dma_start(out=w_sb[:, q], in_=w_by_chunk[q])
+        nc.sync.dma_start(out=g1_sb[:, GROUP:B], in_=g1[GROUP:B].rearrange("b j c -> j b c"))
+        s2_all = keep.tile([P, 1], BF16)
+        nc.sync.dma_start(out=s2_all[:], in_=s2.partition_broadcast(P))
+        a_raw = keep.tile([P, B, PACK * J], BF16)
+        nc.sync.dma_start(out=a_raw[0:R], in_=adj.rearrange("b o (r t) w -> r (b o) (t w)", t=PACK))
+        nc.sync.dma_start(
+            out=a_raw[R:P],
+            in_=spatial_adj.rearrange("k (r t) w -> (k r) (t w)", t=PACK).unsqueeze(1).to_broadcast([P - R, B, PACK * J]),
+        )
+        nc.sync.dma_start(out=res1_sb[:], in_=res1.rearrange("b w c -> w b c"))
+        gamma = keep.tile([P, C], BF16)
+        beta = keep.tile([P, C], BF16)
+        nc.sync.dma_start(out=gamma[:], in_=norm2_g.partition_broadcast(P))
+        nc.sync.dma_start(out=beta[:], in_=norm2_b.partition_broadcast(P))
+
+        ident_f32 = keep.tile([P, P], F32)
+        make_identity(nc, ident_f32[:])
+        ident_bf16 = keep.tile([P, P], BF16)
+        make_identity(nc, ident_bf16[:])
+        joint_order = keep.tile([P, P], F32)
+        nc.vector.tensor_copy(
+            out=joint_order[:].rearrange("p (a r e) -> p a r e", a=2, e=2),
+            in_=ident_f32[:].rearrange("p (r a e) -> p a r e", a=2, e=2),
+        )
+        minus_half = keep.tile([P, 1], F32)
+        nc.vector.memset(minus_half[:], -0.5)
+        gain = keep.tile([P, 1], F32)
+        nc.vector.memset(gain[:], 1.0)
+
+        g1_grouped = keep.tile([P, B, J, PACK], BF16, align_bytes=64)
+        g1_codes = keep.tile([P, N_GROUPS, GROUP * J], U32, align_bytes=64)
+        g1_scales = keep.tile([P, N_GROUPS, GROUP * J], U8, align_bytes=64)
+        w_grouped = keep.tile([P, CHUNKS, K, P, PACK], BF16, align_bytes=64)
+        w_codes = keep.tile([P, CHUNKS, K * P], U32, align_bytes=64)
+        w_scales = keep.tile([P, CHUNKS, K * P], U8, align_bytes=64)
+        a_grouped = keep.tile([P, B, J, PACK], BF16, align_bytes=64)
+        a_codes = keep.tile([P, B, J], U32, align_bytes=64)
+        a_scales = keep.tile([P, B, J], U8, align_bytes=64)
+
+        def transpose_two(rows_0, rows_1, selector, every_second):
+            bank = psum_tr.tile([P, 2, 2, P], F32, tag="bank")
+            for i, rows in enumerate((rows_0, rows_1)):
+                words = rows.bitcast(F32)
+                for u in range(2):
+                    block = words[:, u : 2 * P : 2] if every_second else words[:, u * P : (u + 1) * P]
+                    nc.tensor.transpose(bank[:, i, u, :], block, selector[:])
+            return bank
+
+        def group_two(on_scalar, grouped, bank):
+            out_words = (
+                grouped.rearrange("p i n e -> p (i n e)").bitcast(F32).rearrange("p (i n u) -> p i n u", i=2, u=2)
+            )
+            in_words = bank[:].rearrange("p i u n -> p i n u")
+            if on_scalar:
+                nc.scalar.copy(out=out_words, in_=in_words)
+            else:
+                nc.vector.tensor_copy(out=out_words, in_=in_words)
+
+        def spread_g1(g):
+            for pair in range(GROUP // 2):
+                b = g * GROUP + 2 * pair
+                bank = transpose_two(g1_sb[:, b, :], g1_sb[:, b + 1, :], joint_order, True)
+                group_two(pair % 2 == 1, g1_grouped[:, b : b + 2], bank)
+
+        def quantise_g1(g):
+            nc.vector.quantize_mx(
+                out=g1_codes[:, g, :].bitcast(FP8X4),
+                scales=g1_scales[:, g, :],
+                in_=g1_grouped[:, g * GROUP : (g + 1) * GROUP].rearrange("p b n e -> p (b n e)"),
+            )
+
+        def spread_w(q):
+            for pair in range(K // 2):
+                k = 2 * pair
+                bank = transpose_two(w_sb[:, q, k, :], w_sb[:, q, k + 1, :], ident_f32, True)
+                group_two(pair % 2 == 1, w_grouped[:, q, k : k + 2], bank)
+
+        def quantise_w(q):
+            nc.vector.quantize_mx(
+                out=w_codes[:, q, :].bitcast(FP8X4),
+                scales=w_scales[:, q, :],
+                in_=w_grouped[:, q].rearrange("p k m e -> p (k m e)"),
+            )
+
+        def prepare_a():
+            nc.vector.tensor_copy(out=gain[0:R, :], in_=s2_all[0:R, :])
+            halves = [slice(half * B // 2, (half + 1) * B // 2) for half in range(2)]
+            for samples in halves:
+                nc.vector.tensor_scalar(
+                    out=a_grouped[:, samples],
+                    in0=a_raw[:, samples].rearrange("p b (t w) -> p b w t", t=PACK),
+                    scalar1=gain[:, 0:1],
+                    scalar2=None,
+                    op0=ALU.mult,
+                )
+            for samples in halves:
+                nc.vector.quantize_mx(
+                    out=a_codes[:, samples, :].rearrange("p b w -> p (b w)").bitcast(FP8X4),
+                    scales=a_scales[:, samples, :].rearrange("p b w -> p (b w)"),
+                    in_=a_grouped[:, samples].rearrange("p b w t -> p (b w t)"),
+                )
+
+        h_t = {}
+
+        def step1(g, q):
+            if q == 0:
+                h_t_new = per_group.tile([P, GROUP, CHUNKS, C], BF16, tag="h_t")
+                h_t[g] = h_t_new
+            for k in range(K):
+                acc = psum_s1.tile([P, GROUP * J], F32)
+                nc.tensor.matmul_mx(
+                    out=acc[:],
+                    lhsT=w_codes[:, q, k * P : (k + 1) * P].bitcast(FP8X4),
+                    lhsT_scale=w_scales[:, q, k * P : (k + 1) * P],
+                    rhs=g1_codes[:, g, :].bitcast(FP8X4),
+                    rhs_scale=g1_scales[:, g, :],
+                    start=True,
+                    stop=True,
+                )
+                nc.scalar.activation(
+                    out=h_t[g][:, :, q, :].rearrange("p b (a k n) -> p b a k n", a=2, k=K)[:, :, :, k, :],
+                    in_=acc[:].rearrange("p (b a n) -> p b a n", b=GROUP, a=2),
+                    func=ACT.Identity,
+                    bias=bias_col[:, k * CHUNKS + q : k * CHUNKS + q + 1],
+                    scale=1.0,
+                )
+
+        h_banks = {}
+        h_grouped = {}
+        g2 = {}
+        x2 = {}
+        stats = {}
+        mean_var = {}
+        rstd = {}
+        centred = {}
+
+        def transpose_h(b):
+            rows = h_t[b // GROUP][:, b % GROUP]
+            h_banks[b] = [transpose_two(rows[:, 2 * half, :], rows[:, 2 * half + 1, :], ident_f32, False) for half in range(2)]
+
+        def group_h(b):
+            h_grouped_new = per_sample.tile([P, CHUNKS, P, PACK], BF16, align_bytes=64, tag="h_grouped")
+            h_grouped[b] = h_grouped_new
+            for half in range(2):
+                group_two(True, h_grouped_new[:, 2 * half : 2 * half + 2], h_banks[b][half])
+
+        def step2(b):
+            h_codes = per_sample.tile([P, C], U32, align_bytes=64)
+            h_scales = per_sample.tile([P, C], U8, align_bytes=64)
+            nc.vector.quantize_mx(
+                out=h_codes[:].bitcast(FP8X4), scales=h_scales[:], in_=h_grouped[b][:].rearrange("p q c t -> p (q c t)")
+            )
+            g2_new = psum_s2.tile([P, C], F32, tag="g2")
+            g2[b] = g2_new
+            nc.tensor.matmul_mx(
+                out=g2_new[:],
+                lhsT=a_codes[:, b, :].bitcast(FP8X4),
+                lhsT_scale=a_scales[:, b, :],
+                rhs=h_codes[:].bitcast(FP8X4),
+                rhs_scale=h_scales[:],
+                start=True,
+                stop=True,
+            )
+
+        def residual(b):
+            x2_new = per_sample.tile([P, C], F32, tag="x2")
+            x2[b] = x2_new
+            nc.vector.tensor_tensor(out=x2_new[:], in0=g2[b][:], in1=res1_sb[:, b, :], op=ALU.add)
+            nc.sync.dma_start(out=out_0[b], in_=x2_new[:])
+
+        def statistics(b):
+            stats_new = per_sample.tile([P, 6], F32, tag="stats")
+            stats[b] = stats_new
+            nc.vector.bn_stats(out=stats_new[:], in_=x2[b][:])
+
+        def mean_and_rstd(b):
+            mean_var_new = per_sample.tile([P, 2], F32, tag="mean_var")
+            mean_var[b] = mean_var_new
+            nc.vector.bn_aggr(out=mean_var_new[:], in_=stats[b][:])
+            var_eps = per_sample.tile([P, 1], F32)
+            nc.gpsimd.tensor_scalar(out=var_eps[:], in0=mean_var_new[:, 1:2], scalar1=EPS, scalar2=None, op0=ALU.add)
+            rstd_new = per_sample.tile([P, 1], F32, tag="rstd")
+            rstd[b] = rstd_new
+            nc.gpsimd.tensor_tensor(out=rstd_new[:], in0=var_eps[:], in1=minus_half[:], op=ALU.pow)
+
+        def centre(b):
+            centred_new = per_sample.tile([P, C], F32, tag="centred")
+            centred[b] = centred_new
+            nc.vector.scalar_tensor_tensor(
+                out=centred_new[:], in0=x2[b][:], scalar=mean_var[b][:, 0:1], in1=gamma[:], op0=ALU.subtract, op1=ALU.mult
+            )
+
+        def scale_and_shift(b):
+            xn = per_sample.tile([P, C], F32)
+            nc.vector.scalar_tensor_tensor(
+                out=xn[:], in0=centred[b][:], scalar=rstd[b][:, 0:1], in1=beta[:], op0=ALU.mult, op1=ALU.add
+            )
+            nc.sync.dma_start(out=out_1[b], in_=xn[:])
+
+
+        spread_g1(0)
+        spread_w(0)
+        quantise_g1(0)
+        quantise_w(0)
+        spread_w(1)
+        bias_ps = psum_tr.tile([P, P], BF16, tag="bank")
+        nc.tensor.transpose(bias_ps[:], bias_rows[:], ident_bf16[:])
+        bias_col = keep.tile([P, K * CHUNKS], F32)
+        nc.vector.tensor_copy(out=bias_col[:], in_=bias_ps[:, 0 : K * CHUNKS])
+        for q in range(CHUNKS):
+            if q + 1 < CHUNKS:
+                quantise_w(q + 1)
+            if q + 1 == CHUNKS:
+                for g in range(1, N_GROUPS):
+                    quantise_g1(g)
+            step1(0, q)
+            if q + 2 < CHUNKS:
+                spread_w(q + 2)
+            if q + 2 == CHUNKS:
+                for g in range(1, N_GROUPS):
+                    spread_g1(g)
+        prepare_a()
+
+        chunks_a_round = CHUNKS // GROUP
+        transpose_h(0)
+        for b in range(B + 2):
+            if b < B:
+                group_h(b)
+                if b // GROUP + 1 < N_GROUPS:
+                    for q in range((b % GROUP) * chunks_a_round, (b % GROUP + 1) * chunks_a_round):
+                        step1(b // GROUP + 1, q)
+                if b + 1 < B:
+                    transpose_h(b + 1)
+                step2(b)
+            if 0 <= b - 1 < B:
+                residual(b - 1)
+            if 0 <= b - 2:
+                centre(b - 2)
+            if 0 <= b - 1 < B:
+                statistics(b - 1)
+            if 0 <= b - 2:
+                scale_and_shift(b - 2)
+            if 0 <= b - 1 < B:
+                mean_and_rstd(b - 1)

@@ -19,7 +19,7 @@ C = 512
 K = 4
 R = J // PACK
 CHUNKS = C // P
-GROUP = 4
+GROUP = 2
 N_GROUPS = B // GROUP
 EPS = 1e-5
 
@@ -33,7 +33,7 @@ def tile_block_attention_guide_pb_kernel(
     with ExitStack() as ctx:
         ctx.enter_context(tc.manual_schedule())
         keep = ctx.enter_context(tc.tile_pool(name="keep", bufs=1))
-        per_group = ctx.enter_context(tc.tile_pool(name="per_group", bufs=2))
+        per_group = ctx.enter_context(tc.tile_pool(name="per_group", bufs=3))
         per_sample = ctx.enter_context(tc.tile_pool(name="per_sample", bufs=3))
         psum_tr = ctx.enter_context(tc.psum_pool(name="psum_tr", bufs=4))
         psum_s1 = ctx.enter_context(tc.psum_pool(name="psum_s1", bufs=3))
@@ -43,14 +43,19 @@ def tile_block_attention_guide_pb_kernel(
         w_sb = keep.tile([P, CHUNKS, K, C], BF16)
         res1_sb = keep.tile([P, B, C], BF16)
         w_by_chunk = conv2_w.rearrange("(k q p) c -> q p k c", k=K, q=CHUNKS)
-        nc.sync.dma_start(out=g1_sb[:, 0:GROUP], in_=g1[0:GROUP].rearrange("b j c -> j b c"))
-        nc.sync.dma_start(out=w_sb[:, 0], in_=w_by_chunk[0])
+
+        def load_g1(first, last):
+            nc.sync.dma_start(out=g1_sb[:, first:last], in_=g1[first:last].rearrange("b j c -> j b c"))
+
+        load_g1(0, GROUP)
+        nc.sync.dma_start(out=w_sb[:, 0, 0:2], in_=w_by_chunk[0][:, 0:2])
+        nc.sync.dma_start(out=w_sb[:, 0, 2:4], in_=w_by_chunk[0][:, 2:4])
         bias_rows = keep.tile([P, P], BF16)
         nc.vector.memset(bias_rows[:], 0.0)
         nc.sync.dma_start(out=bias_rows[0 : K * CHUNKS, :], in_=conv2_b.rearrange("(i p) -> i p", p=P))
         for q in range(1, CHUNKS):
             nc.sync.dma_start(out=w_sb[:, q], in_=w_by_chunk[q])
-        nc.sync.dma_start(out=g1_sb[:, GROUP:B], in_=g1[GROUP:B].rearrange("b j c -> j b c"))
+        load_g1(GROUP, 2 * GROUP)
         s2_all = keep.tile([P, 1], BF16)
         nc.sync.dma_start(out=s2_all[:], in_=s2.partition_broadcast(P))
         a_raw = keep.tile([P, B, PACK * J], BF16)
@@ -59,6 +64,7 @@ def tile_block_attention_guide_pb_kernel(
             out=a_raw[R:P],
             in_=spatial_adj.rearrange("k (r t) w -> (k r) (t w)", t=PACK).unsqueeze(1).to_broadcast([P - R, B, PACK * J]),
         )
+        load_g1(2 * GROUP, B)
         nc.sync.dma_start(out=res1_sb[:], in_=res1.rearrange("b w c -> w b c"))
         gamma = keep.tile([P, C], BF16)
         beta = keep.tile([P, C], BF16)
@@ -74,10 +80,11 @@ def tile_block_attention_guide_pb_kernel(
             out=joint_order[:].rearrange("p (a r e) -> p a r e", a=2, e=2),
             in_=ident_f32[:].rearrange("p (r a e) -> p a r e", a=2, e=2),
         )
-        minus_half = keep.tile([P, 1], F32)
-        nc.vector.memset(minus_half[:], -0.5)
         gain = keep.tile([P, 1], F32)
         nc.vector.memset(gain[:], 1.0)
+        eps = keep.tile([P, 1], F32)
+        nc.vector.memset(eps[:], 0.0)
+        nc.vector.tensor_scalar(out=eps[:], in0=eps[:], scalar1=EPS, scalar2=None, op0=ALU.add)
 
         g1_grouped = keep.tile([P, B, J, PACK], BF16, align_bytes=64)
         g1_codes = keep.tile([P, N_GROUPS, GROUP * J], U32, align_bytes=64)
@@ -108,11 +115,10 @@ def tile_block_attention_guide_pb_kernel(
             else:
                 nc.vector.tensor_copy(out=out_words, in_=in_words)
 
-        def spread_g1(g):
-            for pair in range(GROUP // 2):
-                b = g * GROUP + 2 * pair
-                bank = transpose_two(g1_sb[:, b, :], g1_sb[:, b + 1, :], joint_order, True)
-                group_two(pair % 2 == 1, g1_grouped[:, b : b + 2], bank)
+        def spread_g1(g, on_scalar):
+            b = g * GROUP
+            bank = transpose_two(g1_sb[:, b, :], g1_sb[:, b + 1, :], joint_order, True)
+            group_two(on_scalar, g1_grouped[:, b : b + 2], bank)
 
         def quantise_g1(g):
             nc.vector.quantize_mx(
@@ -121,11 +127,10 @@ def tile_block_attention_guide_pb_kernel(
                 in_=g1_grouped[:, g * GROUP : (g + 1) * GROUP].rearrange("p b n e -> p (b n e)"),
             )
 
-        def spread_w(q):
-            for pair in range(K // 2):
-                k = 2 * pair
-                bank = transpose_two(w_sb[:, q, k, :], w_sb[:, q, k + 1, :], ident_f32, True)
-                group_two(pair % 2 == 1, w_grouped[:, q, k : k + 2], bank)
+        def spread_w(q, pair, on_scalar):
+            k = 2 * pair
+            bank = transpose_two(w_sb[:, q, k, :], w_sb[:, q, k + 1, :], ident_f32, True)
+            group_two(on_scalar, w_grouped[:, q, k : k + 2], bank)
 
         def quantise_w(q):
             nc.vector.quantize_mx(
@@ -134,82 +139,100 @@ def tile_block_attention_guide_pb_kernel(
                 in_=w_grouped[:, q].rearrange("p k m e -> p (k m e)"),
             )
 
-        def prepare_a():
+        def set_gain():
             nc.vector.tensor_copy(out=gain[0:R, :], in_=s2_all[0:R, :])
-            halves = [slice(half * B // 2, (half + 1) * B // 2) for half in range(2)]
-            for samples in halves:
-                nc.vector.tensor_scalar(
-                    out=a_grouped[:, samples],
-                    in0=a_raw[:, samples].rearrange("p b (t w) -> p b w t", t=PACK),
-                    scalar1=gain[:, 0:1],
-                    scalar2=None,
-                    op0=ALU.mult,
-                )
-            for samples in halves:
-                nc.vector.quantize_mx(
-                    out=a_codes[:, samples, :].rearrange("p b w -> p (b w)").bitcast(FP8X4),
-                    scales=a_scales[:, samples, :].rearrange("p b w -> p (b w)"),
-                    in_=a_grouped[:, samples].rearrange("p b w t -> p (b w t)"),
-                )
+
+        def group_a(g):
+            samples = slice(g * GROUP, (g + 1) * GROUP)
+            nc.gpsimd.tensor_scalar(
+                out=a_grouped[:, samples],
+                in0=a_raw[:, samples].rearrange("p b (t w) -> p b w t", t=PACK),
+                scalar1=gain[:, 0:1],
+                scalar2=0.0,
+                op0=ALU.mult,
+                op1=ALU.add,
+            )
+
+        def quantise_a(g):
+            samples = slice(g * GROUP, (g + 1) * GROUP)
+            nc.vector.quantize_mx(
+                out=a_codes[:, samples, :].rearrange("p b w -> p (b w)").bitcast(FP8X4),
+                scales=a_scales[:, samples, :].rearrange("p b w -> p (b w)"),
+                in_=a_grouped[:, samples].rearrange("p b w t -> p (b w t)"),
+            )
 
         h_t = {}
 
-        def step1(g, q):
+        def step1(g, q, on_scalar):
             if q == 0:
                 h_t_new = per_group.tile([P, GROUP, CHUNKS, C], BF16, tag="h_t")
                 h_t[g] = h_t_new
-            for k in range(K):
-                acc = psum_s1.tile([P, GROUP * J], F32)
-                nc.tensor.matmul_mx(
-                    out=acc[:],
-                    lhsT=w_codes[:, q, k * P : (k + 1) * P].bitcast(FP8X4),
-                    lhsT_scale=w_scales[:, q, k * P : (k + 1) * P],
-                    rhs=g1_codes[:, g, :].bitcast(FP8X4),
-                    rhs_scale=g1_scales[:, g, :],
-                    start=True,
-                    stop=True,
-                )
-                nc.scalar.activation(
-                    out=h_t[g][:, :, q, :].rearrange("p b (a k n) -> p b a k n", a=2, k=K)[:, :, :, k, :],
-                    in_=acc[:].rearrange("p (b a n) -> p b a n", b=GROUP, a=2),
-                    func=ACT.Identity,
-                    bias=bias_col[:, k * CHUNKS + q : k * CHUNKS + q + 1],
-                    scale=1.0,
-                )
+            for pair in range(K // 2):
+                acc = psum_s1.tile([P, 2, GROUP * J], F32)
+                for i in range(2):
+                    k = 2 * pair + i
+                    nc.tensor.matmul_mx(
+                        out=acc[:, i, :],
+                        lhsT=w_codes[:, q, k * P : (k + 1) * P].bitcast(FP8X4),
+                        lhsT_scale=w_scales[:, q, k * P : (k + 1) * P],
+                        rhs=g1_codes[:, g, :].bitcast(FP8X4),
+                        rhs_scale=g1_scales[:, g, :],
+                        start=True,
+                        stop=True,
+                    )
+                for i in range(2):
+                    k = 2 * pair + i
+                    biased = h_t[g][:, :, q, :].rearrange("p b (a k n) -> p b a k n", a=2, k=K)[:, :, :, k, :]
+                    sums = acc[:, i, :].rearrange("p (b a n) -> p b a n", b=GROUP, a=2)
+                    bias = bias_col[:, k * CHUNKS + q : k * CHUNKS + q + 1]
+                    if on_scalar:
+                        nc.scalar.activation(out=biased, in_=sums, func=ACT.Identity, bias=bias, scale=1.0)
+                    else:
+                        nc.vector.tensor_scalar(out=biased, in0=sums, scalar1=bias, scalar2=None, op0=ALU.add)
 
         h_banks = {}
         h_grouped = {}
         g2 = {}
         x2 = {}
-        stats = {}
-        mean_var = {}
+        row_sums = {}
+        minus_mean = {}
         rstd = {}
         centred = {}
+        h_codes = {}
+        h_scales = {}
 
         def transpose_h(b):
             rows = h_t[b // GROUP][:, b % GROUP]
-            h_banks[b] = [transpose_two(rows[:, 2 * half, :], rows[:, 2 * half + 1, :], ident_f32, False) for half in range(2)]
+            h_banks[b] = [
+                transpose_two(rows[:, 2 * half, :], rows[:, 2 * half + 1, :], ident_f32, False) for half in range(2)
+            ]
 
-        def group_h(b):
-            h_grouped_new = per_sample.tile([P, CHUNKS, P, PACK], BF16, align_bytes=64, tag="h_grouped")
-            h_grouped[b] = h_grouped_new
-            for half in range(2):
-                group_two(True, h_grouped_new[:, 2 * half : 2 * half + 2], h_banks[b][half])
+        def group_h(b, half, on_scalar):
+            if half == 0:
+                h_grouped_new = per_sample.tile([P, CHUNKS, P, PACK], BF16, align_bytes=64, tag="h_grouped")
+                h_grouped[b] = h_grouped_new
+            group_two(on_scalar, h_grouped[b][:, 2 * half : 2 * half + 2], h_banks[b][half])
+
+        def quantise_h(b):
+            h_codes_new = per_sample.tile([P, C], U32, align_bytes=64, tag="h_codes")
+            h_scales_new = per_sample.tile([P, C], U8, align_bytes=64, tag="h_scales")
+            h_codes[b] = h_codes_new
+            h_scales[b] = h_scales_new
+            nc.vector.quantize_mx(
+                out=h_codes_new[:].bitcast(FP8X4),
+                scales=h_scales_new[:],
+                in_=h_grouped[b][:].rearrange("p q c t -> p (q c t)"),
+            )
 
         def step2(b):
-            h_codes = per_sample.tile([P, C], U32, align_bytes=64)
-            h_scales = per_sample.tile([P, C], U8, align_bytes=64)
-            nc.vector.quantize_mx(
-                out=h_codes[:].bitcast(FP8X4), scales=h_scales[:], in_=h_grouped[b][:].rearrange("p q c t -> p (q c t)")
-            )
             g2_new = psum_s2.tile([P, C], F32, tag="g2")
             g2[b] = g2_new
             nc.tensor.matmul_mx(
                 out=g2_new[:],
                 lhsT=a_codes[:, b, :].bitcast(FP8X4),
                 lhsT_scale=a_scales[:, b, :],
-                rhs=h_codes[:].bitcast(FP8X4),
-                rhs_scale=h_scales[:],
+                rhs=h_codes[b][:].bitcast(FP8X4),
+                rhs_scale=h_scales[b][:],
                 start=True,
                 stop=True,
             )
@@ -217,29 +240,48 @@ def tile_block_attention_guide_pb_kernel(
         def residual(b):
             x2_new = per_sample.tile([P, C], F32, tag="x2")
             x2[b] = x2_new
-            nc.vector.tensor_tensor(out=x2_new[:], in0=g2[b][:], in1=res1_sb[:, b, :], op=ALU.add)
+            sums_new = per_sample.tile([P, 1], F32, tag="sums")
+            row_sums[b] = sums_new
+            nc.vector.scalar_tensor_tensor(
+                out=x2_new[:],
+                in0=g2[b][:],
+                scalar=1.0,
+                in1=res1_sb[:, b, :],
+                op0=ALU.mult,
+                op1=ALU.add,
+                accum_out=sums_new[:],
+            )
             nc.sync.dma_start(out=out_0[b], in_=x2_new[:])
 
-        def statistics(b):
-            stats_new = per_sample.tile([P, 6], F32, tag="stats")
-            stats[b] = stats_new
-            nc.vector.bn_stats(out=stats_new[:], in_=x2[b][:])
+        def mean(b):
+            minus_mean_new = per_sample.tile([P, 1], F32, tag="minus_mean")
+            minus_mean[b] = minus_mean_new
+            nc.vector.tensor_scalar(
+                out=minus_mean_new[:], in0=row_sums[b][:], scalar1=-1.0 / C, scalar2=None, op0=ALU.mult
+            )
 
-        def mean_and_rstd(b):
-            mean_var_new = per_sample.tile([P, 2], F32, tag="mean_var")
-            mean_var[b] = mean_var_new
-            nc.vector.bn_aggr(out=mean_var_new[:], in_=stats[b][:])
-            var_eps = per_sample.tile([P, 1], F32)
-            nc.gpsimd.tensor_scalar(out=var_eps[:], in0=mean_var_new[:, 1:2], scalar1=EPS, scalar2=None, op0=ALU.add)
+        def variance(b):
+            squares = per_sample.tile([P, C], F32)
+            total = per_sample.tile([P, 1], F32)
+            nc.scalar.activation(
+                out=squares[:],
+                in_=x2[b][:],
+                func=ACT.Square,
+                bias=minus_mean[b][:, 0:1],
+                scale=1.0,
+                accum_out=total[:],
+            )
             rstd_new = per_sample.tile([P, 1], F32, tag="rstd")
             rstd[b] = rstd_new
-            nc.gpsimd.tensor_tensor(out=rstd_new[:], in0=var_eps[:], in1=minus_half[:], op=ALU.pow)
+            nc.scalar.activation(
+                out=rstd_new[:], in_=total[:], func=ACT.Abs_reciprocal_sqrt, bias=eps[:, 0:1], scale=1.0 / C
+            )
 
         def centre(b):
             centred_new = per_sample.tile([P, C], F32, tag="centred")
             centred[b] = centred_new
             nc.vector.scalar_tensor_tensor(
-                out=centred_new[:], in0=x2[b][:], scalar=mean_var[b][:, 0:1], in1=gamma[:], op0=ALU.subtract, op1=ALU.mult
+                out=centred_new[:], in0=x2[b][:], scalar=minus_mean[b][:, 0:1], in1=gamma[:], op0=ALU.add, op1=ALU.mult
             )
 
         def scale_and_shift(b):
@@ -249,48 +291,70 @@ def tile_block_attention_guide_pb_kernel(
             )
             nc.sync.dma_start(out=out_1[b], in_=xn[:])
 
-
-        spread_g1(0)
-        spread_w(0)
+        spread_g1(0, False)
+        spread_w(0, 0, True)
         quantise_g1(0)
+        spread_w(0, 1, False)
+        spread_w(1, 0, True)
         quantise_w(0)
-        spread_w(1)
+        spread_w(1, 1, False)
         bias_ps = psum_tr.tile([P, P], BF16, tag="bank")
         nc.tensor.transpose(bias_ps[:], bias_rows[:], ident_bf16[:])
         bias_col = keep.tile([P, K * CHUNKS], F32)
         nc.vector.tensor_copy(out=bias_col[:], in_=bias_ps[:, 0 : K * CHUNKS])
-        for q in range(CHUNKS):
-            if q + 1 < CHUNKS:
-                quantise_w(q + 1)
-            if q + 1 == CHUNKS:
-                for g in range(1, N_GROUPS):
-                    quantise_g1(g)
-            step1(0, q)
-            if q + 2 < CHUNKS:
-                spread_w(q + 2)
-            if q + 2 == CHUNKS:
-                for g in range(1, N_GROUPS):
-                    spread_g1(g)
-        prepare_a()
-
-        chunks_a_round = CHUNKS // GROUP
+        quantise_w(1)
+        step1(0, 0, True)
+        spread_w(2, 0, True)
+        spread_w(2, 1, False)
+        step1(0, 1, True)
+        spread_w(3, 0, True)
+        quantise_w(2)
+        spread_w(3, 1, False)
+        step1(0, 2, True)
+        quantise_w(3)
+        set_gain()
+        for g in range(N_GROUPS):
+            group_a(g)
+        spread_g1(1, False)
+        step1(0, 3, True)
+        quantise_g1(1)
+        spread_g1(2, False)
         transpose_h(0)
+        step1(1, 0, False)
+        group_h(0, 0, True)
+        group_h(0, 1, True)
+        step1(1, 1, False)
+        step1(1, 2, True)
+        quantise_g1(2)
+        spread_g1(3, False)
+        step1(1, 3, True)
+        quantise_a(0)
+
         for b in range(B + 2):
+            if b + 1 < B:
+                transpose_h(b + 1)
+                group_h(b + 1, 0, True)
             if b < B:
-                group_h(b)
-                if b // GROUP + 1 < N_GROUPS:
-                    for q in range((b % GROUP) * chunks_a_round, (b % GROUP + 1) * chunks_a_round):
-                        step1(b // GROUP + 1, q)
-                if b + 1 < B:
-                    transpose_h(b + 1)
+                quantise_h(b)
+            if b == 0:
+                quantise_g1(3)
+            g, half = divmod(b + 4, GROUP)
+            if g < N_GROUPS:
+                for q in range(half * CHUNKS // GROUP, (half + 1) * CHUNKS // GROUP):
+                    step1(g, q, True)
+            if b < B:
                 step2(b)
             if 0 <= b - 1 < B:
                 residual(b - 1)
-            if 0 <= b - 2:
+            if 0 <= b - 2 < B:
                 centre(b - 2)
             if 0 <= b - 1 < B:
-                statistics(b - 1)
-            if 0 <= b - 2:
+                mean(b - 1)
+            if b + 1 < B:
+                group_h(b + 1, 1, b >= 4)
+            if 0 <= b - 2 < B:
                 scale_and_shift(b - 2)
             if 0 <= b - 1 < B:
-                mean_and_rstd(b - 1)
+                variance(b - 1)
+            if 0 < b + 1 < N_GROUPS:
+                quantise_a(b + 1)

@@ -86,6 +86,11 @@ def tile_block_attention_guide_pb_kernel(
         nc.vector.memset(eps[:], 0.0)
         nc.vector.tensor_scalar(out=eps[:], in0=eps[:], scalar1=EPS, scalar2=None, op0=ALU.add)
 
+        warm_scalar = keep.tile([P, 1], F32)
+        nc.scalar.activation(out=warm_scalar[:], in_=gain[:], func=ACT.Abs_reciprocal_sqrt, bias=eps[:, 0:1], scale=1.0)
+        zeros = keep.tile([P, C], BF16)
+        nc.vector.memset(zeros[:], 0.0)
+
         g1_grouped = keep.tile([P, B, J, PACK], BF16, align_bytes=64)
         g1_codes = keep.tile([P, N_GROUPS, GROUP * J], U32, align_bytes=64)
         g1_scales = keep.tile([P, N_GROUPS, GROUP * J], U8, align_bytes=64)
@@ -291,13 +296,23 @@ def tile_block_attention_guide_pb_kernel(
             )
             nc.sync.dma_start(out=out_1[b], in_=xn[:])
 
+        def keep_clock(times):
+            idle = psum_s2.tile([P, C], F32, tag="g2")
+            for i in range(times):
+                nc.tensor.matmul(out=idle[:], lhsT=zeros[:, 0:P], rhs=zeros[:], start=True, stop=True)
+
+        keep_clock(4)
         spread_g1(0, False)
         spread_w(0, 0, True)
         quantise_g1(0)
+        keep_clock(1)
         spread_w(0, 1, False)
+        keep_clock(2)
         spread_w(1, 0, True)
         quantise_w(0)
+        keep_clock(1)
         spread_w(1, 1, False)
+        keep_clock(1)
         bias_ps = psum_tr.tile([P, P], BF16, tag="bank")
         nc.tensor.transpose(bias_ps[:], bias_rows[:], ident_bf16[:])
         bias_col = keep.tile([P, K * CHUNKS], F32)
@@ -305,10 +320,12 @@ def tile_block_attention_guide_pb_kernel(
         quantise_w(1)
         step1(0, 0, True)
         spread_w(2, 0, True)
+        keep_clock(1)
         spread_w(2, 1, False)
         step1(0, 1, True)
         spread_w(3, 0, True)
         quantise_w(2)
+        keep_clock(1)
         spread_w(3, 1, False)
         step1(0, 2, True)
         quantise_w(3)

@@ -39,6 +39,9 @@ def tile_block_attention_guide_pb_kernel(
         psum_s1 = ctx.enter_context(tc.psum_pool(name="psum_s1", bufs=3))
         psum_s2 = ctx.enter_context(tc.psum_pool(name="psum_s2", bufs=1))
 
+        zeros = keep.tile([P, C], BF16)
+        nc.vector.memset(zeros[:].bitcast(U32), 0)
+
         g1_sb = keep.tile([P, B, C], BF16)
         w_sb = keep.tile([P, CHUNKS, K, C], BF16)
         res1_sb = keep.tile([P, B, C], BF16)
@@ -88,8 +91,6 @@ def tile_block_attention_guide_pb_kernel(
 
         warm_scalar = keep.tile([P, 1], F32)
         nc.scalar.activation(out=warm_scalar[:], in_=gain[:], func=ACT.Abs_reciprocal_sqrt, bias=eps[:, 0:1], scale=1.0)
-        zeros = keep.tile([P, C], BF16)
-        nc.vector.memset(zeros[:], 0.0)
 
         g1_grouped = keep.tile([P, B, J, PACK], BF16, align_bytes=64)
         g1_codes = keep.tile([P, N_GROUPS, GROUP * J], U32, align_bytes=64)
@@ -147,16 +148,15 @@ def tile_block_attention_guide_pb_kernel(
         def set_gain():
             nc.vector.tensor_copy(out=gain[0:R, :], in_=s2_all[0:R, :])
 
-        def group_a(g):
+        def group_a(g, on_scalar):
             samples = slice(g * GROUP, (g + 1) * GROUP)
-            nc.gpsimd.tensor_scalar(
-                out=a_grouped[:, samples],
-                in0=a_raw[:, samples].rearrange("p b (t w) -> p b w t", t=PACK),
-                scalar1=gain[:, 0:1],
-                scalar2=0.0,
-                op0=ALU.mult,
-                op1=ALU.add,
-            )
+            raw = a_raw[:, samples].rearrange("p b (t w) -> p b w t", t=PACK)
+            if on_scalar:
+                nc.scalar.activation(out=a_grouped[:, samples], in_=raw, func=ACT.Copy, scale=gain[:, 0:1])
+            else:
+                nc.vector.tensor_scalar(
+                    out=a_grouped[:, samples], in0=raw, scalar1=gain[:, 0:1], scalar2=None, op0=ALU.mult
+                )
 
         def quantise_a(g):
             samples = slice(g * GROUP, (g + 1) * GROUP)
@@ -201,6 +201,7 @@ def tile_block_attention_guide_pb_kernel(
         x2 = {}
         row_sums = {}
         minus_mean = {}
+        totals = {}
         rstd = {}
         centred = {}
         h_codes = {}
@@ -276,10 +277,13 @@ def tile_block_attention_guide_pb_kernel(
                 scale=1.0,
                 accum_out=total[:],
             )
+            totals[b] = total
+
+        def inverse_deviation(b):
             rstd_new = per_sample.tile([P, 1], F32, tag="rstd")
             rstd[b] = rstd_new
             nc.scalar.activation(
-                out=rstd_new[:], in_=total[:], func=ACT.Abs_reciprocal_sqrt, bias=eps[:, 0:1], scale=1.0 / C
+                out=rstd_new[:], in_=totals[b][:], func=ACT.Abs_reciprocal_sqrt, bias=eps[:, 0:1], scale=1.0 / C
             )
 
         def centre(b):
@@ -301,38 +305,33 @@ def tile_block_attention_guide_pb_kernel(
             for i in range(times):
                 nc.tensor.matmul(out=idle[:], lhsT=zeros[:, 0:P], rhs=zeros[:], start=True, stop=True)
 
-        keep_clock(4)
-        spread_g1(0, False)
-        spread_w(0, 0, True)
+        keep_clock(3)
+        spread_g1(0, True)
+        spread_w(0, 0, False)
         quantise_g1(0)
         keep_clock(1)
-        spread_w(0, 1, False)
-        keep_clock(2)
-        spread_w(1, 0, True)
+        spread_w(0, 1, True)
         quantise_w(0)
         keep_clock(1)
-        spread_w(1, 1, False)
-        keep_clock(1)
+        spread_w(1, 0, False)
+        spread_w(1, 1, True)
         bias_ps = psum_tr.tile([P, P], BF16, tag="bank")
         nc.tensor.transpose(bias_ps[:], bias_rows[:], ident_bf16[:])
         bias_col = keep.tile([P, K * CHUNKS], F32)
         nc.vector.tensor_copy(out=bias_col[:], in_=bias_ps[:, 0 : K * CHUNKS])
         quantise_w(1)
         step1(0, 0, True)
-        spread_w(2, 0, True)
-        keep_clock(1)
-        spread_w(2, 1, False)
+        spread_w(2, 0, False)
+        spread_w(2, 1, True)
         step1(0, 1, True)
-        spread_w(3, 0, True)
         quantise_w(2)
-        keep_clock(1)
-        spread_w(3, 1, False)
+        spread_w(3, 0, False)
+        spread_w(3, 1, True)
         step1(0, 2, True)
-        quantise_w(3)
         set_gain()
-        for g in range(N_GROUPS):
-            group_a(g)
+        quantise_w(3)
         spread_g1(1, False)
+        group_a(0, False)
         step1(0, 3, True)
         quantise_g1(1)
         spread_g1(2, False)
@@ -355,23 +354,27 @@ def tile_block_attention_guide_pb_kernel(
                 quantise_h(b)
             if b == 0:
                 quantise_g1(3)
+            if 0 <= b - 2:
+                inverse_deviation(b - 2)
             g, half = divmod(b + 4, GROUP)
             if g < N_GROUPS:
                 for q in range(half * CHUNKS // GROUP, (half + 1) * CHUNKS // GROUP):
                     step1(g, q, True)
             if b < B:
                 step2(b)
-            if 0 <= b - 1 < B:
-                residual(b - 1)
             if 0 <= b - 2 < B:
                 centre(b - 2)
             if 0 <= b - 1 < B:
-                mean(b - 1)
-            if b + 1 < B:
-                group_h(b + 1, 1, b >= 4)
+                residual(b - 1)
             if 0 <= b - 2 < B:
                 scale_and_shift(b - 2)
             if 0 <= b - 1 < B:
+                mean(b - 1)
+            if b < N_GROUPS - 1:
+                group_a(b + 1, False)
+            if b + 1 < B:
+                group_h(b + 1, 1, b >= 4)
+            if 0 <= b - 1 < B:
                 variance(b - 1)
-            if 0 < b + 1 < N_GROUPS:
+            if b < N_GROUPS - 1:
                 quantise_a(b + 1)

@@ -19,7 +19,7 @@ C = 512
 K = 4
 R = J // PACK
 CHUNKS = C // P
-GROUP = 2
+GROUP = 4
 N_GROUPS = B // GROUP
 EPS = 1e-5
 
@@ -33,11 +33,10 @@ def tile_block_attention_guide_pb_kernel(
     with ExitStack() as ctx:
         ctx.enter_context(tc.manual_schedule())
         keep = ctx.enter_context(tc.tile_pool(name="keep", bufs=1))
-        per_group = ctx.enter_context(tc.tile_pool(name="per_group", bufs=3))
+        per_group = ctx.enter_context(tc.tile_pool(name="per_group", bufs=2))
         per_sample = ctx.enter_context(tc.tile_pool(name="per_sample", bufs=3))
         psum_tr = ctx.enter_context(tc.psum_pool(name="psum_tr", bufs=4))
-        psum_s1 = ctx.enter_context(tc.psum_pool(name="psum_s1", bufs=3))
-        psum_s2 = ctx.enter_context(tc.psum_pool(name="psum_s2", bufs=1))
+        psum_acc = ctx.enter_context(tc.psum_pool(name="psum_acc", bufs=4))
 
         zeros = keep.tile([P, C], BF16)
         nc.vector.memset(zeros[:].bitcast(U32), 0)
@@ -50,15 +49,16 @@ def tile_block_attention_guide_pb_kernel(
         def load_g1(first, last):
             nc.sync.dma_start(out=g1_sb[:, first:last], in_=g1[first:last].rearrange("b j c -> j b c"))
 
-        load_g1(0, GROUP)
+        load_g1(0, 2)
         nc.sync.dma_start(out=w_sb[:, 0, 0:2], in_=w_by_chunk[0][:, 0:2])
+        load_g1(2, 4)
         nc.sync.dma_start(out=w_sb[:, 0, 2:4], in_=w_by_chunk[0][:, 2:4])
         bias_rows = keep.tile([P, P], BF16)
         nc.vector.memset(bias_rows[:], 0.0)
         nc.sync.dma_start(out=bias_rows[0 : K * CHUNKS, :], in_=conv2_b.rearrange("(i p) -> i p", p=P))
         for q in range(1, CHUNKS):
             nc.sync.dma_start(out=w_sb[:, q], in_=w_by_chunk[q])
-        load_g1(GROUP, 2 * GROUP)
+        load_g1(4, 6)
         s2_all = keep.tile([P, 1], BF16)
         nc.sync.dma_start(out=s2_all[:], in_=s2.partition_broadcast(P))
         a_raw = keep.tile([P, B, PACK * J], BF16)
@@ -67,7 +67,7 @@ def tile_block_attention_guide_pb_kernel(
             out=a_raw[R:P],
             in_=spatial_adj.rearrange("k (r t) w -> (k r) (t w)", t=PACK).unsqueeze(1).to_broadcast([P - R, B, PACK * J]),
         )
-        load_g1(2 * GROUP, B)
+        load_g1(6, 8)
         nc.sync.dma_start(out=res1_sb[:], in_=res1.rearrange("b w c -> w b c"))
         gamma = keep.tile([P, C], BF16)
         beta = keep.tile([P, C], BF16)
@@ -121,16 +121,18 @@ def tile_block_attention_guide_pb_kernel(
             else:
                 nc.vector.tensor_copy(out=out_words, in_=in_words)
 
-        def spread_g1(g, on_scalar):
-            b = g * GROUP
+        def spread_g1(pair, on_scalar):
+            b = 2 * pair
             bank = transpose_two(g1_sb[:, b, :], g1_sb[:, b + 1, :], joint_order, True)
             group_two(on_scalar, g1_grouped[:, b : b + 2], bank)
 
-        def quantise_g1(g):
+        def quantise_g1(pair):
+            b = 2 * pair
+            columns = slice(b % GROUP * J, (b % GROUP + 2) * J)
             nc.vector.quantize_mx(
-                out=g1_codes[:, g, :].bitcast(FP8X4),
-                scales=g1_scales[:, g, :],
-                in_=g1_grouped[:, g * GROUP : (g + 1) * GROUP].rearrange("p b n e -> p (b n e)"),
+                out=g1_codes[:, b // GROUP, columns].bitcast(FP8X4),
+                scales=g1_scales[:, b // GROUP, columns],
+                in_=g1_grouped[:, b : b + 2].rearrange("p b n e -> p (b n e)"),
             )
 
         def spread_w(q, pair, on_scalar):
@@ -148,8 +150,8 @@ def tile_block_attention_guide_pb_kernel(
         def set_gain():
             nc.vector.tensor_copy(out=gain[0:R, :], in_=s2_all[0:R, :])
 
-        def group_a(g, on_scalar):
-            samples = slice(g * GROUP, (g + 1) * GROUP)
+        def group_a(pair, on_scalar):
+            samples = slice(2 * pair, 2 * pair + 2)
             raw = a_raw[:, samples].rearrange("p b (t w) -> p b w t", t=PACK)
             if on_scalar:
                 nc.scalar.activation(out=a_grouped[:, samples], in_=raw, func=ACT.Copy, scale=gain[:, 0:1])
@@ -158,8 +160,8 @@ def tile_block_attention_guide_pb_kernel(
                     out=a_grouped[:, samples], in0=raw, scalar1=gain[:, 0:1], scalar2=None, op0=ALU.mult
                 )
 
-        def quantise_a(g):
-            samples = slice(g * GROUP, (g + 1) * GROUP)
+        def quantise_a(pair):
+            samples = slice(2 * pair, 2 * pair + 2)
             nc.vector.quantize_mx(
                 out=a_codes[:, samples, :].rearrange("p b w -> p (b w)").bitcast(FP8X4),
                 scales=a_scales[:, samples, :].rearrange("p b w -> p (b w)"),
@@ -168,32 +170,28 @@ def tile_block_attention_guide_pb_kernel(
 
         h_t = {}
 
-        def step1(g, q, on_scalar):
-            if q == 0:
+        def step1(g, q, slices, on_scalar):
+            if g not in h_t:
                 h_t_new = per_group.tile([P, GROUP, CHUNKS, C], BF16, tag="h_t")
                 h_t[g] = h_t_new
-            for pair in range(K // 2):
-                acc = psum_s1.tile([P, 2, GROUP * J], F32)
-                for i in range(2):
-                    k = 2 * pair + i
-                    nc.tensor.matmul_mx(
-                        out=acc[:, i, :],
-                        lhsT=w_codes[:, q, k * P : (k + 1) * P].bitcast(FP8X4),
-                        lhsT_scale=w_scales[:, q, k * P : (k + 1) * P],
-                        rhs=g1_codes[:, g, :].bitcast(FP8X4),
-                        rhs_scale=g1_scales[:, g, :],
-                        start=True,
-                        stop=True,
-                    )
-                for i in range(2):
-                    k = 2 * pair + i
-                    biased = h_t[g][:, :, q, :].rearrange("p b (a k n) -> p b a k n", a=2, k=K)[:, :, :, k, :]
-                    sums = acc[:, i, :].rearrange("p (b a n) -> p b a n", b=GROUP, a=2)
-                    bias = bias_col[:, k * CHUNKS + q : k * CHUNKS + q + 1]
-                    if on_scalar:
-                        nc.scalar.activation(out=biased, in_=sums, func=ACT.Identity, bias=bias, scale=1.0)
-                    else:
-                        nc.vector.tensor_scalar(out=biased, in0=sums, scalar1=bias, scalar2=None, op0=ALU.add)
+            for k in slices:
+                acc = psum_acc.tile([P, GROUP * J], F32, tag="acc")
+                nc.tensor.matmul_mx(
+                    out=acc[:],
+                    lhsT=w_codes[:, q, k * P : (k + 1) * P].bitcast(FP8X4),
+                    lhsT_scale=w_scales[:, q, k * P : (k + 1) * P],
+                    rhs=g1_codes[:, g, :].bitcast(FP8X4),
+                    rhs_scale=g1_scales[:, g, :],
+                    start=True,
+                    stop=True,
+                )
+                biased = h_t[g][:, :, q, :].rearrange("p b (a k n) -> p b a k n", a=2, k=K)[:, :, :, k, :]
+                sums = acc[:].rearrange("p (b a n) -> p b a n", b=GROUP, a=2)
+                bias = bias_col[:, k * CHUNKS + q : k * CHUNKS + q + 1]
+                if on_scalar:
+                    nc.scalar.activation(out=biased, in_=sums, func=ACT.Identity, bias=bias, scale=1.0)
+                else:
+                    nc.vector.tensor_scalar(out=biased, in0=sums, scalar1=bias, scalar2=None, op0=ALU.add)
 
         h_banks = {}
         h_grouped = {}
@@ -214,7 +212,7 @@ def tile_block_attention_guide_pb_kernel(
             ]
 
         def group_h(b, half, on_scalar):
-            if half == 0:
+            if b not in h_grouped:
                 h_grouped_new = per_sample.tile([P, CHUNKS, P, PACK], BF16, align_bytes=64, tag="h_grouped")
                 h_grouped[b] = h_grouped_new
             group_two(on_scalar, h_grouped[b][:, 2 * half : 2 * half + 2], h_banks[b][half])
@@ -231,7 +229,7 @@ def tile_block_attention_guide_pb_kernel(
             )
 
         def step2(b):
-            g2_new = psum_s2.tile([P, C], F32, tag="g2")
+            g2_new = psum_acc.tile([P, C], F32, tag="acc")
             g2[b] = g2_new
             nc.tensor.matmul_mx(
                 out=g2_new[:],
@@ -301,80 +299,76 @@ def tile_block_attention_guide_pb_kernel(
             nc.sync.dma_start(out=out_1[b], in_=xn[:])
 
         def keep_clock(times):
-            idle = psum_s2.tile([P, C], F32, tag="g2")
+            idle = psum_acc.tile([P, C], F32, tag="acc")
             for i in range(times):
                 nc.tensor.matmul(out=idle[:], lhsT=zeros[:, 0:P], rhs=zeros[:], start=True, stop=True)
 
         keep_clock(3)
         spread_g1(0, True)
         spread_w(0, 0, False)
+        spread_g1(1, True)
         quantise_g1(0)
-        keep_clock(1)
-        spread_w(0, 1, True)
+        spread_w(0, 1, False)
+        quantise_g1(1)
         quantise_w(0)
         keep_clock(1)
-        spread_w(1, 0, False)
-        spread_w(1, 1, True)
+        spread_w(1, 0, True)
+        spread_w(1, 1, False)
         bias_ps = psum_tr.tile([P, P], BF16, tag="bank")
         nc.tensor.transpose(bias_ps[:], bias_rows[:], ident_bf16[:])
         bias_col = keep.tile([P, K * CHUNKS], F32)
         nc.vector.tensor_copy(out=bias_col[:], in_=bias_ps[:, 0 : K * CHUNKS])
         quantise_w(1)
-        step1(0, 0, True)
-        spread_w(2, 0, False)
-        spread_w(2, 1, True)
-        step1(0, 1, True)
+        step1(0, 0, range(0, 3), True)
+        step1(0, 0, range(3, 4), False)
+        spread_w(2, 0, True)
+        spread_w(2, 1, False)
         quantise_w(2)
-        spread_w(3, 0, False)
-        spread_w(3, 1, True)
-        step1(0, 2, True)
-        set_gain()
+        step1(0, 1, range(0, 3), True)
+        step1(0, 1, range(3, 4), False)
+        spread_w(3, 0, True)
+        spread_w(3, 1, False)
         quantise_w(3)
-        spread_g1(1, False)
-        group_a(0, False)
-        step1(0, 3, True)
-        quantise_g1(1)
+        step1(0, 2, range(0, 3), True)
+        step1(0, 2, range(3, 4), False)
+        set_gain()
         spread_g1(2, False)
-        transpose_h(0)
-        step1(1, 0, False)
-        group_h(0, 0, True)
-        group_h(0, 1, True)
-        step1(1, 1, False)
-        step1(1, 2, True)
+        group_a(0, False)
         quantise_g1(2)
-        spread_g1(3, False)
-        step1(1, 3, True)
+        step1(0, 3, range(0, 2), True)
+        step1(0, 3, range(2, 4), False)
+        spread_g1(3, True)
         quantise_a(0)
+        quantise_g1(3)
 
-        for b in range(B + 2):
+        for b in range(-1, B + 1):
             if b + 1 < B:
                 transpose_h(b + 1)
                 group_h(b + 1, 0, True)
-            if b < B:
+            if 0 <= b < B:
                 quantise_h(b)
-            if b == 0:
-                quantise_g1(3)
-            if 0 <= b - 2:
-                inverse_deviation(b - 2)
-            g, half = divmod(b + 4, GROUP)
-            if g < N_GROUPS:
-                for q in range(half * CHUNKS // GROUP, (half + 1) * CHUNKS // GROUP):
-                    step1(g, q, True)
-            if b < B:
-                step2(b)
-            if 0 <= b - 2 < B:
-                centre(b - 2)
-            if 0 <= b - 1 < B:
-                residual(b - 1)
-            if 0 <= b - 2 < B:
-                scale_and_shift(b - 2)
-            if 0 <= b - 1 < B:
-                mean(b - 1)
-            if b < N_GROUPS - 1:
-                group_a(b + 1, False)
-            if b + 1 < B:
-                group_h(b + 1, 1, b >= 4)
-            if 0 <= b - 1 < B:
+            if 0 <= b - 1:
+                centre(b - 1)
                 variance(b - 1)
-            if b < N_GROUPS - 1:
+            if b + 1 < CHUNKS:
+                step1(1, b + 1, range(0, 1), True)
+            if 0 <= b - 1:
+                inverse_deviation(b - 1)
+            if b + 1 < CHUNKS:
+                step1(1, b + 1, range(1, 3), True)
+            if 0 <= b < B:
+                step2(b)
+            if b + 1 < CHUNKS:
+                step1(1, b + 1, range(3, 4), True)
+            if b + 1 < B:
+                group_h(b + 1, 1, b >= 3)
+            if 0 <= b < 3:
+                group_a(b + 1, False)
+            if 0 <= b < B:
+                residual(b)
+            if 0 <= b - 1:
+                scale_and_shift(b - 1)
+            if 0 <= b < B:
+                mean(b)
+            if 0 <= b < 3:
                 quantise_a(b + 1)

@@ -41,24 +41,20 @@ def tile_block_attention_guide_pb_kernel(
         zeros = keep.tile([P, C], BF16)
         nc.vector.memset(zeros[:].bitcast(U32), 0)
 
-        g1_sb = keep.tile([P, B, C], BF16)
-        w_sb = keep.tile([P, CHUNKS, K, C], BF16)
+        g1_sb = keep.tile([P, N_GROUPS, PACK, C], BF16)
+        w_sb = keep.tile([P, K, CHUNKS, C], BF16)
         res1_sb = keep.tile([P, B, C], BF16)
-        w_by_chunk = conv2_w.rearrange("(k q p) c -> q p k c", k=K, q=CHUNKS)
-
-        def load_g1(first, last):
-            nc.sync.dma_start(out=g1_sb[:, first:last], in_=g1[first:last].rearrange("b j c -> j b c"))
-
-        load_g1(0, 2)
-        nc.sync.dma_start(out=w_sb[:, 0, 0:2], in_=w_by_chunk[0][:, 0:2])
-        load_g1(2, 4)
-        nc.sync.dma_start(out=w_sb[:, 0, 2:4], in_=w_by_chunk[0][:, 2:4])
-        bias_rows = keep.tile([P, P], BF16)
-        nc.vector.memset(bias_rows[:], 0.0)
-        nc.sync.dma_start(out=bias_rows[0 : K * CHUNKS, :], in_=conv2_b.rearrange("(i p) -> i p", p=P))
-        for q in range(1, CHUNKS):
-            nc.sync.dma_start(out=w_sb[:, q], in_=w_by_chunk[q])
-        load_g1(4, 6)
+        g1_rows = g1.rearrange("(g s) (r i) c -> g (s r) i c", s=GROUP, i=PACK)
+        w_rows = conv2_w.rearrange("(k p q) c -> k p q c", k=K, q=CHUNKS)
+        halves = (slice(0, 2), slice(2, 4))
+        for half in halves:
+            nc.sync.dma_start(out=g1_sb[:, 0, half], in_=g1_rows[0][:, half])
+            nc.sync.dma_start(out=w_sb[:, 0, half], in_=w_rows[0][:, half])
+        bias_bf16 = keep.tile([P, K, CHUNKS], BF16)
+        nc.sync.dma_start(out=bias_bf16[:], in_=conv2_b.rearrange("(k p q) -> p k q", k=K, q=CHUNKS))
+        for k in range(1, K):
+            nc.sync.dma_start(out=w_sb[:, k], in_=w_rows[k])
+        nc.sync.dma_start(out=g1_sb[:, 1], in_=g1_rows[1])
         s2_all = keep.tile([P, 1], BF16)
         nc.sync.dma_start(out=s2_all[:], in_=s2.partition_broadcast(P))
         a_raw = keep.tile([P, B, PACK * J], BF16)
@@ -67,7 +63,6 @@ def tile_block_attention_guide_pb_kernel(
             out=a_raw[R:P],
             in_=spatial_adj.rearrange("k (r t) w -> (k r) (t w)", t=PACK).unsqueeze(1).to_broadcast([P - R, B, PACK * J]),
         )
-        load_g1(6, 8)
         nc.sync.dma_start(out=res1_sb[:], in_=res1.rearrange("b w c -> w b c"))
         gamma = keep.tile([P, C], BF16)
         beta = keep.tile([P, C], BF16)
@@ -76,13 +71,6 @@ def tile_block_attention_guide_pb_kernel(
 
         ident_f32 = keep.tile([P, P], F32)
         make_identity(nc, ident_f32[:])
-        ident_bf16 = keep.tile([P, P], BF16)
-        make_identity(nc, ident_bf16[:])
-        joint_order = keep.tile([P, P], F32)
-        nc.vector.tensor_copy(
-            out=joint_order[:].rearrange("p (a r e) -> p a r e", a=2, e=2),
-            in_=ident_f32[:].rearrange("p (r a e) -> p a r e", a=2, e=2),
-        )
         gain = keep.tile([P, 1], F32)
         nc.vector.memset(gain[:], 1.0)
         eps = keep.tile([P, 1], F32)
@@ -92,59 +80,65 @@ def tile_block_attention_guide_pb_kernel(
         warm_scalar = keep.tile([P, 1], F32)
         nc.scalar.activation(out=warm_scalar[:], in_=gain[:], func=ACT.Abs_reciprocal_sqrt, bias=eps[:, 0:1], scale=1.0)
 
-        g1_grouped = keep.tile([P, B, J, PACK], BF16, align_bytes=64)
+        g1_grouped = keep.tile([P, N_GROUPS, 2, 2 * P, PACK], BF16, align_bytes=64)
         g1_codes = keep.tile([P, N_GROUPS, GROUP * J], U32, align_bytes=64)
         g1_scales = keep.tile([P, N_GROUPS, GROUP * J], U8, align_bytes=64)
-        w_grouped = keep.tile([P, CHUNKS, K, P, PACK], BF16, align_bytes=64)
-        w_codes = keep.tile([P, CHUNKS, K * P], U32, align_bytes=64)
-        w_scales = keep.tile([P, CHUNKS, K * P], U8, align_bytes=64)
+        w_grouped = keep.tile([P, K, CHUNKS, P, PACK], BF16, align_bytes=64)
+        w_codes = keep.tile([P, K, CHUNKS * P], U32, align_bytes=64)
+        w_scales = keep.tile([P, K, CHUNKS * P], U8, align_bytes=64)
         a_grouped = keep.tile([P, B, J, PACK], BF16, align_bytes=64)
         a_codes = keep.tile([P, B, J], U32, align_bytes=64)
         a_scales = keep.tile([P, B, J], U8, align_bytes=64)
 
-        def transpose_two(rows_0, rows_1, selector, every_second):
+        def transpose_two(rows, every_second):
             bank = psum_tr.tile([P, 2, 2, P], F32, tag="bank")
-            for i, rows in enumerate((rows_0, rows_1)):
-                words = rows.bitcast(F32)
+            for i in range(2):
+                words = rows[:, i, :].bitcast(F32)
                 for u in range(2):
                     block = words[:, u : 2 * P : 2] if every_second else words[:, u * P : (u + 1) * P]
-                    nc.tensor.transpose(bank[:, i, u, :], block, selector[:])
+                    nc.tensor.transpose(bank[:, i, u, :], block, ident_f32[:])
             return bank
 
-        def group_two(on_scalar, grouped, bank):
-            out_words = (
-                grouped.rearrange("p i n e -> p (i n e)").bitcast(F32).rearrange("p (i n u) -> p i n u", i=2, u=2)
-            )
-            in_words = bank[:].rearrange("p i u n -> p i n u")
+        def copy_words(on_scalar, out_words, in_words):
             if on_scalar:
                 nc.scalar.copy(out=out_words, in_=in_words)
             else:
                 nc.vector.tensor_copy(out=out_words, in_=in_words)
 
-        def spread_g1(pair, on_scalar):
-            b = 2 * pair
-            bank = transpose_two(g1_sb[:, b, :], g1_sb[:, b + 1, :], joint_order, True)
-            group_two(on_scalar, g1_grouped[:, b : b + 2], bank)
-
-        def quantise_g1(pair):
-            b = 2 * pair
-            columns = slice(b % GROUP * J, (b % GROUP + 2) * J)
-            nc.vector.quantize_mx(
-                out=g1_codes[:, b // GROUP, columns].bitcast(FP8X4),
-                scales=g1_scales[:, b // GROUP, columns],
-                in_=g1_grouped[:, b : b + 2].rearrange("p b n e -> p (b n e)"),
+        def group_two(on_scalar, grouped, bank):
+            out_words = grouped.rearrange("p i n e -> p (i n e)").bitcast(F32)
+            copy_words(
+                on_scalar,
+                out_words.rearrange("p (i n u) -> p i n u", i=2, u=2),
+                bank[:].rearrange("p i u n -> p i n u"),
             )
 
-        def spread_w(q, pair, on_scalar):
-            k = 2 * pair
-            bank = transpose_two(w_sb[:, q, k, :], w_sb[:, q, k + 1, :], ident_f32, True)
-            group_two(on_scalar, w_grouped[:, q, k : k + 2], bank)
+        def spread_g1(g, a, on_scalar):
+            bank = transpose_two(g1_sb[:, g, 2 * a : 2 * a + 2, :], True)
+            out_words = g1_grouped[:, g, a].rearrange("p n e -> p (n e)").bitcast(F32)
+            copy_words(
+                on_scalar,
+                out_words.rearrange("p (n e u) -> p n e u", e=2, u=2),
+                bank[:].rearrange("p e u n -> p n e u"),
+            )
 
-        def quantise_w(q):
+        def quantise_g1(g, a):
+            columns = slice(a * 2 * P, (a + 1) * 2 * P)
             nc.vector.quantize_mx(
-                out=w_codes[:, q, :].bitcast(FP8X4),
-                scales=w_scales[:, q, :],
-                in_=w_grouped[:, q].rearrange("p k m e -> p (k m e)"),
+                out=g1_codes[:, g, columns].bitcast(FP8X4),
+                scales=g1_scales[:, g, columns],
+                in_=g1_grouped[:, g, a].rearrange("p n e -> p (n e)"),
+            )
+
+        def spread_w(k, half, on_scalar):
+            bank = transpose_two(w_sb[:, k, halves[half], :], True)
+            group_two(on_scalar, w_grouped[:, k, halves[half]], bank)
+
+        def quantise_w(k):
+            nc.vector.quantize_mx(
+                out=w_codes[:, k, :].bitcast(FP8X4),
+                scales=w_scales[:, k, :],
+                in_=w_grouped[:, k].rearrange("p q m e -> p (q m e)"),
             )
 
         def set_gain():
@@ -170,24 +164,24 @@ def tile_block_attention_guide_pb_kernel(
 
         h_t = {}
 
-        def step1(g, q, slices, on_scalar):
+        def step1(g, k, chunks, on_scalar):
             if g not in h_t:
                 h_t_new = per_group.tile([P, GROUP, CHUNKS, C], BF16, tag="h_t")
                 h_t[g] = h_t_new
-            for k in slices:
+            for q in chunks:
                 acc = psum_acc.tile([P, GROUP * J], F32, tag="acc")
                 nc.tensor.matmul_mx(
                     out=acc[:],
-                    lhsT=w_codes[:, q, k * P : (k + 1) * P].bitcast(FP8X4),
-                    lhsT_scale=w_scales[:, q, k * P : (k + 1) * P],
+                    lhsT=w_codes[:, k, q * P : (q + 1) * P].bitcast(FP8X4),
+                    lhsT_scale=w_scales[:, k, q * P : (q + 1) * P],
                     rhs=g1_codes[:, g, :].bitcast(FP8X4),
                     rhs_scale=g1_scales[:, g, :],
                     start=True,
                     stop=True,
                 )
                 biased = h_t[g][:, :, q, :].rearrange("p b (a k n) -> p b a k n", a=2, k=K)[:, :, :, k, :]
-                sums = acc[:].rearrange("p (b a n) -> p b a n", b=GROUP, a=2)
-                bias = bias_col[:, k * CHUNKS + q : k * CHUNKS + q + 1]
+                sums = acc[:].rearrange("p (a b n) -> p b a n", b=GROUP, a=2)
+                bias = bias_col[:, k, q : q + 1]
                 if on_scalar:
                     nc.scalar.activation(out=biased, in_=sums, func=ACT.Identity, bias=bias, scale=1.0)
                 else:
@@ -206,10 +200,7 @@ def tile_block_attention_guide_pb_kernel(
         h_scales = {}
 
         def transpose_h(b):
-            rows = h_t[b // GROUP][:, b % GROUP]
-            h_banks[b] = [
-                transpose_two(rows[:, 2 * half, :], rows[:, 2 * half + 1, :], ident_f32, False) for half in range(2)
-            ]
+            h_banks[b] = [transpose_two(h_t[b // GROUP][:, b % GROUP, half, :], False) for half in halves]
 
         def group_h(b, half, on_scalar):
             if b not in h_grouped:
@@ -247,10 +238,10 @@ def tile_block_attention_guide_pb_kernel(
             sums_new = per_sample.tile([P, 1], F32, tag="sums")
             row_sums[b] = sums_new
             nc.vector.scalar_tensor_tensor(
-                out=x2_new[:],
-                in0=g2[b][:],
+                out=x2_new[:].rearrange("p (n q) -> p n q", q=CHUNKS),
+                in0=g2[b][:].rearrange("p (q n) -> p n q", q=CHUNKS),
                 scalar=1.0,
-                in1=res1_sb[:, b, :],
+                in1=res1_sb[:, b, :].rearrange("p (n q) -> p n q", q=CHUNKS),
                 op0=ALU.mult,
                 op1=ALU.add,
                 accum_out=sums_new[:],
@@ -304,20 +295,18 @@ def tile_block_attention_guide_pb_kernel(
                 nc.tensor.matmul(out=idle[:], lhsT=zeros[:, 0:P], rhs=zeros[:], start=True, stop=True)
 
         keep_clock(3)
-        spread_g1(0, True)
+        spread_g1(0, 0, True)
         spread_w(0, 0, False)
-        spread_g1(1, True)
-        quantise_g1(0)
+        spread_g1(0, 1, True)
+        quantise_g1(0, 0)
         spread_w(0, 1, False)
-        quantise_g1(1)
+        quantise_g1(0, 1)
         quantise_w(0)
         keep_clock(1)
         spread_w(1, 0, True)
         spread_w(1, 1, False)
-        bias_ps = psum_tr.tile([P, P], BF16, tag="bank")
-        nc.tensor.transpose(bias_ps[:], bias_rows[:], ident_bf16[:])
-        bias_col = keep.tile([P, K * CHUNKS], F32)
-        nc.vector.tensor_copy(out=bias_col[:], in_=bias_ps[:, 0 : K * CHUNKS])
+        bias_col = keep.tile([P, K, CHUNKS], F32)
+        nc.vector.tensor_copy(out=bias_col[:], in_=bias_bf16[:])
         quantise_w(1)
         step1(0, 0, range(0, 3), True)
         step1(0, 0, range(3, 4), False)
@@ -332,14 +321,14 @@ def tile_block_attention_guide_pb_kernel(
         step1(0, 2, range(0, 3), True)
         step1(0, 2, range(3, 4), False)
         set_gain()
-        spread_g1(2, False)
+        spread_g1(1, 0, False)
         group_a(0, False)
-        quantise_g1(2)
+        quantise_g1(1, 0)
         step1(0, 3, range(0, 2), True)
         step1(0, 3, range(2, 4), False)
-        spread_g1(3, True)
+        spread_g1(1, 1, True)
         quantise_a(0)
-        quantise_g1(3)
+        quantise_g1(1, 1)
 
         for b in range(-1, B + 1):
             if b + 1 < B:

@@ -164,28 +164,32 @@ def tile_block_attention_guide_pb_kernel(
 
         h_t = {}
 
-        def step1(g, k, chunks, on_scalar):
+        acc = {}
+
+        def multiply(g, k, q):
+            acc_new = psum_acc.tile([P, GROUP * J], F32, tag="acc")
+            acc[g, k, q] = acc_new
+            nc.tensor.matmul_mx(
+                out=acc_new[:],
+                lhsT=w_codes[:, k, q * P : (q + 1) * P].bitcast(FP8X4),
+                lhsT_scale=w_scales[:, k, q * P : (q + 1) * P],
+                rhs=g1_codes[:, g, :].bitcast(FP8X4),
+                rhs_scale=g1_scales[:, g, :],
+                start=True,
+                stop=True,
+            )
+
+        def add_bias(g, k, q, on_scalar):
             if g not in h_t:
                 h_t_new = per_group.tile([P, GROUP, CHUNKS, C], BF16, tag="h_t")
                 h_t[g] = h_t_new
-            for q in chunks:
-                acc = psum_acc.tile([P, GROUP * J], F32, tag="acc")
-                nc.tensor.matmul_mx(
-                    out=acc[:],
-                    lhsT=w_codes[:, k, q * P : (q + 1) * P].bitcast(FP8X4),
-                    lhsT_scale=w_scales[:, k, q * P : (q + 1) * P],
-                    rhs=g1_codes[:, g, :].bitcast(FP8X4),
-                    rhs_scale=g1_scales[:, g, :],
-                    start=True,
-                    stop=True,
-                )
-                biased = h_t[g][:, :, q, :].rearrange("p b (a k n) -> p b a k n", a=2, k=K)[:, :, :, k, :]
-                sums = acc[:].rearrange("p (a b n) -> p b a n", b=GROUP, a=2)
-                bias = bias_col[:, k, q : q + 1]
-                if on_scalar:
-                    nc.scalar.activation(out=biased, in_=sums, func=ACT.Identity, bias=bias, scale=1.0)
-                else:
-                    nc.vector.tensor_scalar(out=biased, in0=sums, scalar1=bias, scalar2=None, op0=ALU.add)
+            biased = h_t[g][:, :, q, :].rearrange("p b (a k n) -> p b a k n", a=2, k=K)[:, :, :, k, :]
+            sums = acc[g, k, q][:].rearrange("p (a b n) -> p b a n", b=GROUP, a=2)
+            bias = bias_col[:, k, q : q + 1]
+            if on_scalar:
+                nc.scalar.activation(out=biased, in_=sums, func=ACT.Identity, bias=bias, scale=1.0)
+            else:
+                nc.vector.tensor_scalar(out=biased, in0=sums, scalar1=bias, scalar2=None, op0=ALU.add)
 
         h_banks = {}
         h_grouped = {}
@@ -303,61 +307,75 @@ def tile_block_attention_guide_pb_kernel(
         quantise_g1(0, 1)
         quantise_w(0)
         keep_clock(1)
-        spread_w(1, 0, True)
-        spread_w(1, 1, False)
         bias_col = keep.tile([P, K, CHUNKS], F32)
         nc.vector.tensor_copy(out=bias_col[:], in_=bias_bf16[:])
-        quantise_w(1)
-        step1(0, 0, range(0, 3), True)
-        step1(0, 0, range(3, 4), False)
-        spread_w(2, 0, True)
-        spread_w(2, 1, False)
-        quantise_w(2)
-        step1(0, 1, range(0, 3), True)
-        step1(0, 1, range(3, 4), False)
-        spread_w(3, 0, True)
-        spread_w(3, 1, False)
-        quantise_w(3)
-        step1(0, 2, range(0, 3), True)
-        step1(0, 2, range(3, 4), False)
+        for k in range(K):
+            if k + 1 < K:
+                spread_w(k + 1, 0, True)
+                spread_w(k + 1, 1, False)
+            else:
+                spread_g1(1, 0, True)
+                spread_g1(1, 1, False)
+            for q in range(CHUNKS):
+                multiply(0, k, q)
+            for q in range(CHUNKS):
+                add_bias(0, k, q, q > 0)
+            if k + 1 < K:
+                quantise_w(k + 1)
+            else:
+                quantise_g1(1, 0)
+                quantise_g1(1, 1)
+        transpose_h(0)
+        for q in range(2):
+            multiply(1, 0, q)
+        transpose_h(1)
+        for q in range(2, 4):
+            multiply(1, 0, q)
         set_gain()
-        spread_g1(1, 0, False)
         group_a(0, False)
-        quantise_g1(1, 0)
-        step1(0, 3, range(0, 2), True)
-        step1(0, 3, range(2, 4), False)
-        spread_g1(1, 1, True)
+        group_h(0, 0, True)
+        group_h(0, 1, False)
         quantise_a(0)
-        quantise_g1(1, 1)
+        for q in range(CHUNKS):
+            add_bias(1, 0, q, True)
 
-        for b in range(-1, B + 1):
-            if b + 1 < B:
-                transpose_h(b + 1)
-                group_h(b + 1, 0, True)
-            if 0 <= b < B:
+        for b in range(B + 1):
+            more = b + 1 < K
+            if b < B:
                 quantise_h(b)
-            if 0 <= b - 1:
-                centre(b - 1)
-                variance(b - 1)
-            if b + 1 < CHUNKS:
-                step1(1, b + 1, range(0, 1), True)
-            if 0 <= b - 1:
-                inverse_deviation(b - 1)
-            if b + 1 < CHUNKS:
-                step1(1, b + 1, range(1, 3), True)
-            if 0 <= b < B:
-                step2(b)
-            if b + 1 < CHUNKS:
-                step1(1, b + 1, range(3, 4), True)
             if b + 1 < B:
-                group_h(b + 1, 1, b >= 3)
-            if 0 <= b < 3:
+                group_h(b + 1, 0, True)
+                if b >= 3:
+                    group_h(b + 1, 1, True)
+            if b < B:
+                step2(b)
+            if more:
+                for q in range(CHUNKS - 1):
+                    multiply(1, b + 1, q)
+                add_bias(1, b + 1, 0, True)
+            if 1 <= b:
+                mean(b - 1)
+                variance(b - 1)
+            if more:
+                add_bias(1, b + 1, 1, True)
+            if 1 <= b:
+                inverse_deviation(b - 1)
+            if more:
+                multiply(1, b + 1, CHUNKS - 1)
+                add_bias(1, b + 1, 2, True)
+                add_bias(1, b + 1, 3, True)
+            if b + 2 < B:
+                transpose_h(b + 2)
+            if b + 1 < B and b < 3:
+                group_h(b + 1, 1, False)
+            if b < 3:
                 group_a(b + 1, False)
-            if 0 <= b < B:
+            if 2 <= b:
+                scale_and_shift(b - 2)
+            if 1 <= b:
+                centre(b - 1)
+            if b < B:
                 residual(b)
-            if 0 <= b - 1:
-                scale_and_shift(b - 1)
-            if 0 <= b < B:
-                mean(b)
-            if 0 <= b < 3:
+            if b < 3:
                 quantise_a(b + 1)
+        scale_and_shift(B - 1)

@@ -50,11 +50,11 @@ def tile_block_attention_guide_pb_kernel(
         for half in halves:
             nc.sync.dma_start(out=g1_sb[:, 0, half], in_=g1_rows[0][:, half])
             nc.sync.dma_start(out=w_sb[:, 0, half], in_=w_rows[0][:, half])
-        bias_bf16 = keep.tile([P, K, CHUNKS], BF16)
-        nc.sync.dma_start(out=bias_bf16[:], in_=conv2_b.rearrange("(k p q) -> p k q", k=K, q=CHUNKS))
+        bias_rows = keep.tile([P, C], BF16)
+        nc.vector.memset(bias_rows[:].bitcast(U32), 0)
+        nc.sync.dma_start(out=bias_rows[0:K, :], in_=conv2_b.rearrange("(k c) -> k c", k=K))
         for k in range(1, K):
             nc.sync.dma_start(out=w_sb[:, k], in_=w_rows[k])
-        nc.sync.dma_start(out=g1_sb[:, 1], in_=g1_rows[1])
         s2_all = keep.tile([P, 1], BF16)
         nc.sync.dma_start(out=s2_all[:], in_=s2.partition_broadcast(P))
         a_raw = keep.tile([P, B, PACK * J], BF16)
@@ -63,6 +63,7 @@ def tile_block_attention_guide_pb_kernel(
             out=a_raw[R:P],
             in_=spatial_adj.rearrange("k (r t) w -> (k r) (t w)", t=PACK).unsqueeze(1).to_broadcast([P - R, B, PACK * J]),
         )
+        nc.sync.dma_start(out=g1_sb[:, 1], in_=g1_rows[1])
         nc.sync.dma_start(out=res1_sb[:], in_=res1.rearrange("b w c -> w b c"))
         gamma = keep.tile([P, C], BF16)
         beta = keep.tile([P, C], BF16)
@@ -71,6 +72,8 @@ def tile_block_attention_guide_pb_kernel(
 
         ident_f32 = keep.tile([P, P], F32)
         make_identity(nc, ident_f32[:])
+        ident_bf16 = keep.tile([P, P], BF16)
+        make_identity(nc, ident_bf16[:])
         gain = keep.tile([P, 1], F32)
         nc.vector.memset(gain[:], 1.0)
         eps = keep.tile([P, 1], F32)
@@ -114,7 +117,9 @@ def tile_block_attention_guide_pb_kernel(
             )
 
         def spread_g1(g, a, on_scalar):
-            bank = transpose_two(g1_sb[:, g, 2 * a : 2 * a + 2, :], True)
+            group_g1(g, a, transpose_two(g1_sb[:, g, 2 * a : 2 * a + 2, :], True), on_scalar)
+
+        def group_g1(g, a, bank, on_scalar):
             out_words = g1_grouped[:, g, a].rearrange("p n e -> p (n e)").bitcast(F32)
             copy_words(
                 on_scalar,
@@ -134,11 +139,12 @@ def tile_block_attention_guide_pb_kernel(
             bank = transpose_two(w_sb[:, k, halves[half], :], True)
             group_two(on_scalar, w_grouped[:, k, halves[half]], bank)
 
-        def quantise_w(k):
+        def quantise_w(k, chunks):
+            columns = slice(chunks.start * P, chunks.stop * P)
             nc.vector.quantize_mx(
-                out=w_codes[:, k, :].bitcast(FP8X4),
-                scales=w_scales[:, k, :],
-                in_=w_grouped[:, k].rearrange("p q m e -> p (q m e)"),
+                out=w_codes[:, k, columns].bitcast(FP8X4),
+                scales=w_scales[:, k, columns],
+                in_=w_grouped[:, k, chunks].rearrange("p q m e -> p (q m e)"),
             )
 
         def set_gain():
@@ -164,7 +170,14 @@ def tile_block_attention_guide_pb_kernel(
 
         h_t = {}
 
+        bias_col = keep.tile([P, K, CHUNKS], F32)
         acc = {}
+
+        def load_bias():
+            columns = psum_tr.tile([P, CHUNKS, P], BF16, tag="bank")
+            for q in range(CHUNKS):
+                nc.tensor.transpose(columns[:, q, :], bias_rows[:, q:C:CHUNKS], ident_bf16[:])
+            nc.vector.tensor_copy(out=bias_col[:], in_=columns[:, :, 0:K].rearrange("p q k -> p k q"))
 
         def multiply(g, k, q):
             acc_new = psum_acc.tile([P, GROUP * J], F32, tag="acc")
@@ -203,8 +216,9 @@ def tile_block_attention_guide_pb_kernel(
         h_codes = {}
         h_scales = {}
 
-        def transpose_h(b):
-            h_banks[b] = [transpose_two(h_t[b // GROUP][:, b % GROUP, half, :], False) for half in halves]
+        def transpose_h(b, of_halves):
+            for half in of_halves:
+                h_banks.setdefault(b, []).append(transpose_two(h_t[b // GROUP][:, b % GROUP, half, :], False))
 
         def group_h(b, half, on_scalar):
             if b not in h_grouped:
@@ -288,10 +302,18 @@ def tile_block_attention_guide_pb_kernel(
 
         def scale_and_shift(b):
             xn = per_sample.tile([P, C], F32)
-            nc.vector.scalar_tensor_tensor(
-                out=xn[:], in0=centred[b][:], scalar=rstd[b][:, 0:1], in1=beta[:], op0=ALU.mult, op1=ALU.add
-            )
-            nc.sync.dma_start(out=out_1[b], in_=xn[:])
+            pieces = 2 if b + 1 == B else 1
+            for i in range(pieces):
+                columns = slice(i * C // pieces, (i + 1) * C // pieces)
+                nc.vector.scalar_tensor_tensor(
+                    out=xn[:, columns],
+                    in0=centred[b][:, columns],
+                    scalar=rstd[b][:, 0:1],
+                    in1=beta[:, columns],
+                    op0=ALU.mult,
+                    op1=ALU.add,
+                )
+                nc.sync.dma_start(out=out_1[b][:, columns], in_=xn[:, columns])
 
         def keep_clock(times):
             idle = psum_acc.tile([P, C], F32, tag="acc")
@@ -303,52 +325,54 @@ def tile_block_attention_guide_pb_kernel(
         spread_w(0, 0, False)
         spread_g1(0, 1, True)
         quantise_g1(0, 0)
+        quantise_w(0, halves[0])
         spread_w(0, 1, False)
         quantise_g1(0, 1)
-        quantise_w(0)
-        keep_clock(1)
-        bias_col = keep.tile([P, K, CHUNKS], F32)
-        nc.vector.tensor_copy(out=bias_col[:], in_=bias_bf16[:])
-        for k in range(K):
-            if k + 1 < K:
-                spread_w(k + 1, 0, True)
-                spread_w(k + 1, 1, False)
-            else:
-                spread_g1(1, 0, True)
-                spread_g1(1, 1, False)
+        quantise_w(0, halves[1])
+        load_bias()
+        for k in range(K - 1):
+            spread_w(k + 1, 0, True)
+            spread_w(k + 1, 1, False)
             for q in range(CHUNKS):
                 multiply(0, k, q)
             for q in range(CHUNKS):
                 add_bias(0, k, q, q > 0)
-            if k + 1 < K:
-                quantise_w(k + 1)
-            else:
-                quantise_g1(1, 0)
-                quantise_g1(1, 1)
-        transpose_h(0)
+            quantise_w(k + 1, slice(0, CHUNKS))
+            if k == 2:
+                set_gain()
+                group_a(0, False)
+        bank_a = transpose_two(g1_sb[:, 1, 0:2, :], True)
+        bank_b = transpose_two(g1_sb[:, 1, 2:4, :], True)
+        group_g1(1, 0, bank_a, True)
+        group_g1(1, 1, bank_b, True)
+        for q in range(CHUNKS):
+            multiply(0, K - 1, q)
+        for q in range(CHUNKS):
+            add_bias(0, K - 1, q, q > 0)
+        quantise_g1(1, 0)
+        quantise_g1(1, 1)
+        transpose_h(0, halves[0:1])
         for q in range(2):
             multiply(1, 0, q)
-        transpose_h(1)
+        transpose_h(0, halves[1:2])
+        transpose_h(1, halves)
         for q in range(2, 4):
             multiply(1, 0, q)
-        set_gain()
-        group_a(0, False)
         group_h(0, 0, True)
         group_h(0, 1, False)
         quantise_a(0)
         for q in range(CHUNKS):
             add_bias(1, 0, q, True)
 
-        for b in range(B + 1):
+        for b in range(B - 1):
             more = b + 1 < K
-            if b < B:
-                quantise_h(b)
-            if b + 1 < B:
-                group_h(b + 1, 0, True)
-                if b >= 3:
-                    group_h(b + 1, 1, True)
-            if b < B:
-                step2(b)
+            quantise_h(b)
+            group_h(b + 1, 0, True)
+            step2(b)
+            if b + 1 == GROUP:
+                transpose_h(b + 1, halves[1:2])
+            if 3 <= b:
+                group_h(b + 1, 1, True)
             if more:
                 for q in range(CHUNKS - 1):
                     multiply(1, b + 1, q)
@@ -365,8 +389,8 @@ def tile_block_attention_guide_pb_kernel(
                 add_bias(1, b + 1, 2, True)
                 add_bias(1, b + 1, 3, True)
             if b + 2 < B:
-                transpose_h(b + 2)
-            if b + 1 < B and b < 3:
+                transpose_h(b + 2, halves[0:1] if b + 2 == GROUP else halves)
+            if b < 3:
                 group_h(b + 1, 1, False)
             if b < 3:
                 group_a(b + 1, False)
@@ -374,8 +398,21 @@ def tile_block_attention_guide_pb_kernel(
                 scale_and_shift(b - 2)
             if 1 <= b:
                 centre(b - 1)
-            if b < B:
-                residual(b)
+            if b + 2 == B:
+                quantise_h(b + 1)
+            residual(b)
             if b < 3:
                 quantise_a(b + 1)
+        step2(B - 1)
+        scale_and_shift(B - 3)
+        mean(B - 2)
+        variance(B - 2)
+        inverse_deviation(B - 2)
+        residual(B - 1)
+        centre(B - 2)
+        mean(B - 1)
+        variance(B - 1)
+        inverse_deviation(B - 1)
+        scale_and_shift(B - 2)
+        centre(B - 1)
         scale_and_shift(B - 1)

@@ -55,6 +55,7 @@ def tile_block_attention_guide_pb_kernel(
         nc.sync.dma_start(out=bias_rows[0:K, :], in_=conv2_b.rearrange("(k c) -> k c", k=K))
         for k in range(1, K):
             nc.sync.dma_start(out=w_sb[:, k], in_=w_rows[k])
+        nc.sync.dma_start(out=g1_sb[:, 1], in_=g1_rows[1])
         s2_all = keep.tile([P, 1], BF16)
         nc.sync.dma_start(out=s2_all[:], in_=s2.partition_broadcast(P))
         a_raw = keep.tile([P, B, PACK * J], BF16)
@@ -63,7 +64,6 @@ def tile_block_attention_guide_pb_kernel(
             out=a_raw[R:P],
             in_=spatial_adj.rearrange("k (r t) w -> (k r) (t w)", t=PACK).unsqueeze(1).to_broadcast([P - R, B, PACK * J]),
         )
-        nc.sync.dma_start(out=g1_sb[:, 1], in_=g1_rows[1])
         nc.sync.dma_start(out=res1_sb[:], in_=res1.rearrange("b w c -> w b c"))
         gamma = keep.tile([P, C], BF16)
         beta = keep.tile([P, C], BF16)
@@ -330,6 +330,7 @@ def tile_block_attention_guide_pb_kernel(
         quantise_g1(0, 1)
         quantise_w(0, halves[1])
         load_bias()
+        keep_clock(1)
         for k in range(K - 1):
             spread_w(k + 1, 0, True)
             spread_w(k + 1, 1, False)
@@ -338,9 +339,6 @@ def tile_block_attention_guide_pb_kernel(
             for q in range(CHUNKS):
                 add_bias(0, k, q, q > 0)
             quantise_w(k + 1, slice(0, CHUNKS))
-            if k == 2:
-                set_gain()
-                group_a(0, False)
         bank_a = transpose_two(g1_sb[:, 1, 0:2, :], True)
         bank_b = transpose_two(g1_sb[:, 1, 2:4, :], True)
         group_g1(1, 0, bank_a, True)
@@ -358,6 +356,8 @@ def tile_block_attention_guide_pb_kernel(
         transpose_h(1, halves)
         for q in range(2, 4):
             multiply(1, 0, q)
+        set_gain()
+        group_a(0, False)
         group_h(0, 0, True)
         group_h(0, 1, False)
         quantise_a(0)

@@ -320,9 +320,10 @@ def tile_block_attention_guide_pb_kernel(
             for i in range(times):
                 nc.tensor.matmul(out=idle[:], lhsT=zeros[:, 0:P], rhs=zeros[:], start=True, stop=True)
 
-        keep_clock(3)
+        keep_clock(4)
         spread_g1(0, 0, True)
         spread_w(0, 0, False)
+        keep_clock(1)
         spread_g1(0, 1, True)
         quantise_g1(0, 0)
         quantise_w(0, halves[0])
@@ -330,7 +331,7 @@ def tile_block_attention_guide_pb_kernel(
         quantise_g1(0, 1)
         quantise_w(0, halves[1])
         load_bias()
-        keep_clock(1)
+        keep_clock(2)
         for k in range(K - 1):
             spread_w(k + 1, 0, True)
             spread_w(k + 1, 1, False)
@@ -390,6 +391,8 @@ def tile_block_attention_guide_pb_kernel(
                 add_bias(1, b + 1, 3, True)
             if b + 2 < B:
                 transpose_h(b + 2, halves[0:1] if b + 2 == GROUP else halves)
+                if not more:
+                    keep_clock(2)
             if b < 3:
                 group_h(b + 1, 1, False)
             if b < 3:

from contextlib import ExitStack

import concourse.mybir as mybir
from concourse.masks import make_identity

F32 = mybir.dt.float32
BF16 = mybir.dt.bfloat16
U32 = mybir.dt.uint32
U8 = mybir.dt.uint8
FP8X4 = mybir.dt.float8_e4m3fn_x4
ACT = mybir.ActivationFunctionType
ALU = mybir.AluOpType

P = 128
PACK = 4
B = 8
J = 128
C = 512
K = 4
R = J // PACK
CHUNKS = C // P
GROUP = 4
N_GROUPS = B // GROUP
EPS = 1e-5

FLOPS = 2 * B * J * C * K * C + 2 * B * J * K * J * C


def tile_block_attention_guide_pb_kernel(
    tc, g1, res1, adj, spatial_adj, conv2_w, conv2_b, s2, norm2_g, norm2_b, out_0, out_1
):
    nc = tc.nc
    with ExitStack() as ctx:
        ctx.enter_context(tc.manual_schedule())
        keep = ctx.enter_context(tc.tile_pool(name="keep", bufs=1))
        per_group = ctx.enter_context(tc.tile_pool(name="per_group", bufs=2))
        per_sample = ctx.enter_context(tc.tile_pool(name="per_sample", bufs=3))
        psum_tr = ctx.enter_context(tc.psum_pool(name="psum_tr", bufs=4))
        psum_acc = ctx.enter_context(tc.psum_pool(name="psum_acc", bufs=4))

        zeros = keep.tile([P, C], BF16)
        nc.vector.memset(zeros[:].bitcast(U32), 0)

        g1_sb = keep.tile([P, N_GROUPS, PACK, C], BF16)
        w_sb = keep.tile([P, K, CHUNKS, C], BF16)
        res1_sb = keep.tile([P, B, C], BF16)
        g1_rows = g1.rearrange("(g s) (r i) c -> g (s r) i c", s=GROUP, i=PACK)
        w_rows = conv2_w.rearrange("(k p q) c -> k p q c", k=K, q=CHUNKS)
        halves = (slice(0, 2), slice(2, 4))
        for half in halves:
            nc.sync.dma_start(out=g1_sb[:, 0, half], in_=g1_rows[0][:, half])
            nc.sync.dma_start(out=w_sb[:, 0, half], in_=w_rows[0][:, half])
        bias_rows = keep.tile([P, C], BF16)
        nc.vector.memset(bias_rows[:].bitcast(U32), 0)
        nc.sync.dma_start(out=bias_rows[0:K, :], in_=conv2_b.rearrange("(k c) -> k c", k=K))
        for k in range(1, K):
            nc.sync.dma_start(out=w_sb[:, k], in_=w_rows[k])
        nc.sync.dma_start(out=g1_sb[:, 1], in_=g1_rows[1])
        s2_all = keep.tile([P, 1], BF16)
        nc.sync.dma_start(out=s2_all[:], in_=s2.partition_broadcast(P))
        a_raw = keep.tile([P, B, PACK * J], BF16)
        nc.sync.dma_start(out=a_raw[0:R], in_=adj.rearrange("b o (r t) w -> r (b o) (t w)", t=PACK))
        nc.sync.dma_start(
            out=a_raw[R:P],
            in_=spatial_adj.rearrange("k (r t) w -> (k r) (t w)", t=PACK).unsqueeze(1).to_broadcast([P - R, B, PACK * J]),
        )
        nc.sync.dma_start(out=res1_sb[:], in_=res1.rearrange("b w c -> w b c"))
        gamma = keep.tile([P, C], BF16)
        beta = keep.tile([P, C], BF16)
        nc.sync.dma_start(out=gamma[:], in_=norm2_g.partition_broadcast(P))
        nc.sync.dma_start(out=beta[:], in_=norm2_b.partition_broadcast(P))

        ident_f32 = keep.tile([P, P], F32)
        make_identity(nc, ident_f32[:])
        ident_bf16 = keep.tile([P, P], BF16)
        make_identity(nc, ident_bf16[:])
        gain = keep.tile([P, 1], F32)
        nc.vector.memset(gain[:], 1.0)
        eps = keep.tile([P, 1], F32)
        nc.vector.memset(eps[:], 0.0)
        nc.vector.tensor_scalar(out=eps[:], in0=eps[:], scalar1=EPS, scalar2=None, op0=ALU.add)

        warm_scalar = keep.tile([P, 1], F32)
        nc.scalar.activation(out=warm_scalar[:], in_=gain[:], func=ACT.Abs_reciprocal_sqrt, bias=eps[:, 0:1], scale=1.0)

        g1_grouped = keep.tile([P, N_GROUPS, 2, 2 * P, PACK], BF16, align_bytes=64)
        g1_codes = keep.tile([P, N_GROUPS, GROUP * J], U32, align_bytes=64)
        g1_scales = keep.tile([P, N_GROUPS, GROUP * J], U8, align_bytes=64)
        w_grouped = keep.tile([P, K, CHUNKS, P, PACK], BF16, align_bytes=64)
        w_codes = keep.tile([P, K, CHUNKS * P], U32, align_bytes=64)
        w_scales = keep.tile([P, K, CHUNKS * P], U8, align_bytes=64)
        a_grouped = keep.tile([P, B, J, PACK], BF16, align_bytes=64)
        a_codes = keep.tile([P, B, J], U32, align_bytes=64)
        a_scales = keep.tile([P, B, J], U8, align_bytes=64)

        def transpose_two(rows, every_second):
            bank = psum_tr.tile([P, 2, 2, P], F32, tag="bank")
            for i in range(2):
                words = rows[:, i, :].bitcast(F32)
                for u in range(2):
                    block = words[:, u : 2 * P : 2] if every_second else words[:, u * P : (u + 1) * P]
                    nc.tensor.transpose(bank[:, i, u, :], block, ident_f32[:])
            return bank

        def copy_words(on_scalar, out_words, in_words):
            if on_scalar:
                nc.scalar.copy(out=out_words, in_=in_words)
            else:
                nc.vector.tensor_copy(out=out_words, in_=in_words)

        def group_two(on_scalar, grouped, bank):
            out_words = grouped.rearrange("p i n e -> p (i n e)").bitcast(F32)
            copy_words(
                on_scalar,
                out_words.rearrange("p (i n u) -> p i n u", i=2, u=2),
                bank[:].rearrange("p i u n -> p i n u"),
            )

        def spread_g1(g, a, on_scalar):
            group_g1(g, a, transpose_two(g1_sb[:, g, 2 * a : 2 * a + 2, :], True), on_scalar)

        def group_g1(g, a, bank, on_scalar):
            out_words = g1_grouped[:, g, a].rearrange("p n e -> p (n e)").bitcast(F32)
            copy_words(
                on_scalar,
                out_words.rearrange("p (n e u) -> p n e u", e=2, u=2),
                bank[:].rearrange("p e u n -> p n e u"),
            )

        def quantise_g1(g, a):
            columns = slice(a * 2 * P, (a + 1) * 2 * P)
            nc.vector.quantize_mx(
                out=g1_codes[:, g, columns].bitcast(FP8X4),
                scales=g1_scales[:, g, columns],
                in_=g1_grouped[:, g, a].rearrange("p n e -> p (n e)"),
            )

        def spread_w(k, half, on_scalar):
            bank = transpose_two(w_sb[:, k, halves[half], :], True)
            group_two(on_scalar, w_grouped[:, k, halves[half]], bank)

        def quantise_w(k, chunks):
            columns = slice(chunks.start * P, chunks.stop * P)
            nc.vector.quantize_mx(
                out=w_codes[:, k, columns].bitcast(FP8X4),
                scales=w_scales[:, k, columns],
                in_=w_grouped[:, k, chunks].rearrange("p q m e -> p (q m e)"),
            )

        def set_gain():
            nc.vector.tensor_copy(out=gain[0:R, :], in_=s2_all[0:R, :])

        def group_a(pair, on_scalar):
            samples = slice(2 * pair, 2 * pair + 2)
            raw = a_raw[:, samples].rearrange("p b (t w) -> p b w t", t=PACK)
            if on_scalar:
                nc.scalar.activation(out=a_grouped[:, samples], in_=raw, func=ACT.Copy, scale=gain[:, 0:1])
            else:
                nc.vector.tensor_scalar(
                    out=a_grouped[:, samples], in0=raw, scalar1=gain[:, 0:1], scalar2=None, op0=ALU.mult
                )

        def quantise_a(pair):
            samples = slice(2 * pair, 2 * pair + 2)
            nc.vector.quantize_mx(
                out=a_codes[:, samples, :].rearrange("p b w -> p (b w)").bitcast(FP8X4),
                scales=a_scales[:, samples, :].rearrange("p b w -> p (b w)"),
                in_=a_grouped[:, samples].rearrange("p b w t -> p (b w t)"),
            )

        h_t = {}

        bias_col = keep.tile([P, K, CHUNKS], F32)
        acc = {}

        def load_bias():
            columns = psum_tr.tile([P, CHUNKS, P], BF16, tag="bank")
            for q in range(CHUNKS):
                nc.tensor.transpose(columns[:, q, :], bias_rows[:, q:C:CHUNKS], ident_bf16[:])
            nc.vector.tensor_copy(out=bias_col[:], in_=columns[:, :, 0:K].rearrange("p q k -> p k q"))

        def multiply(g, k, q):
            acc_new = psum_acc.tile([P, GROUP * J], F32, tag="acc")
            acc[g, k, q] = acc_new
            nc.tensor.matmul_mx(
                out=acc_new[:],
                lhsT=w_codes[:, k, q * P : (q + 1) * P].bitcast(FP8X4),
                lhsT_scale=w_scales[:, k, q * P : (q + 1) * P],
                rhs=g1_codes[:, g, :].bitcast(FP8X4),
                rhs_scale=g1_scales[:, g, :],
                start=True,
                stop=True,
            )

        def add_bias(g, k, q, on_scalar):
            if g not in h_t:
                h_t_new = per_group.tile([P, GROUP, CHUNKS, C], BF16, tag="h_t")
                h_t[g] = h_t_new
            biased = h_t[g][:, :, q, :].rearrange("p b (a k n) -> p b a k n", a=2, k=K)[:, :, :, k, :]
            sums = acc[g, k, q][:].rearrange("p (a b n) -> p b a n", b=GROUP, a=2)
            bias = bias_col[:, k, q : q + 1]
            if on_scalar:
                nc.scalar.activation(out=biased, in_=sums, func=ACT.Identity, bias=bias, scale=1.0)
            else:
                nc.vector.tensor_scalar(out=biased, in0=sums, scalar1=bias, scalar2=None, op0=ALU.add)

        h_banks = {}
        h_grouped = {}
        g2 = {}
        x2 = {}
        row_sums = {}
        minus_mean = {}
        totals = {}
        rstd = {}
        centred = {}
        h_codes = {}
        h_scales = {}

        def transpose_h(b, of_halves):
            for half in of_halves:
                h_banks.setdefault(b, []).append(transpose_two(h_t[b // GROUP][:, b % GROUP, half, :], False))

        def group_h(b, half, on_scalar):
            if b not in h_grouped:
                h_grouped_new = per_sample.tile([P, CHUNKS, P, PACK], BF16, align_bytes=64, tag="h_grouped")
                h_grouped[b] = h_grouped_new
            group_two(on_scalar, h_grouped[b][:, 2 * half : 2 * half + 2], h_banks[b][half])

        def quantise_h(b):
            h_codes_new = per_sample.tile([P, C], U32, align_bytes=64, tag="h_codes")
            h_scales_new = per_sample.tile([P, C], U8, align_bytes=64, tag="h_scales")
            h_codes[b] = h_codes_new
            h_scales[b] = h_scales_new
            nc.vector.quantize_mx(
                out=h_codes_new[:].bitcast(FP8X4),
                scales=h_scales_new[:],
                in_=h_grouped[b][:].rearrange("p q c t -> p (q c t)"),
            )

        def step2(b):
            g2_new = psum_acc.tile([P, C], F32, tag="acc")
            g2[b] = g2_new
            nc.tensor.matmul_mx(
                out=g2_new[:],
                lhsT=a_codes[:, b, :].bitcast(FP8X4),
                lhsT_scale=a_scales[:, b, :],
                rhs=h_codes[b][:].bitcast(FP8X4),
                rhs_scale=h_scales[b][:],
                start=True,
                stop=True,
            )

        def residual(b):
            x2_new = per_sample.tile([P, C], F32, tag="x2")
            x2[b] = x2_new
            sums_new = per_sample.tile([P, 1], F32, tag="sums")
            row_sums[b] = sums_new
            nc.vector.scalar_tensor_tensor(
                out=x2_new[:].rearrange("p (n q) -> p n q", q=CHUNKS),
                in0=g2[b][:].rearrange("p (q n) -> p n q", q=CHUNKS),
                scalar=1.0,
                in1=res1_sb[:, b, :].rearrange("p (n q) -> p n q", q=CHUNKS),
                op0=ALU.mult,
                op1=ALU.add,
                accum_out=sums_new[:],
            )
            nc.sync.dma_start(out=out_0[b], in_=x2_new[:])

        def mean(b):
            minus_mean_new = per_sample.tile([P, 1], F32, tag="minus_mean")
            minus_mean[b] = minus_mean_new
            nc.vector.tensor_scalar(
                out=minus_mean_new[:], in0=row_sums[b][:], scalar1=-1.0 / C, scalar2=None, op0=ALU.mult
            )

        def variance(b):
            squares = per_sample.tile([P, C], F32)
            total = per_sample.tile([P, 1], F32)
            nc.scalar.activation(
                out=squares[:],
                in_=x2[b][:],
                func=ACT.Square,
                bias=minus_mean[b][:, 0:1],
                scale=1.0,
                accum_out=total[:],
            )
            totals[b] = total

        def inverse_deviation(b):
            rstd_new = per_sample.tile([P, 1], F32, tag="rstd")
            rstd[b] = rstd_new
            nc.scalar.activation(
                out=rstd_new[:], in_=totals[b][:], func=ACT.Abs_reciprocal_sqrt, bias=eps[:, 0:1], scale=1.0 / C
            )

        def centre(b):
            centred_new = per_sample.tile([P, C], F32, tag="centred")
            centred[b] = centred_new
            nc.vector.scalar_tensor_tensor(
                out=centred_new[:], in0=x2[b][:], scalar=minus_mean[b][:, 0:1], in1=gamma[:], op0=ALU.add, op1=ALU.mult
            )

        def scale_and_shift(b):
            xn = per_sample.tile([P, C], F32)
            pieces = 2 if b + 1 == B else 1
            for i in range(pieces):
                columns = slice(i * C // pieces, (i + 1) * C // pieces)
                nc.vector.scalar_tensor_tensor(
                    out=xn[:, columns],
                    in0=centred[b][:, columns],
                    scalar=rstd[b][:, 0:1],
                    in1=beta[:, columns],
                    op0=ALU.mult,
                    op1=ALU.add,
                )
                nc.sync.dma_start(out=out_1[b][:, columns], in_=xn[:, columns])

        def keep_clock(times):
            idle = psum_acc.tile([P, C], F32, tag="acc")
            for i in range(times):
                nc.tensor.matmul(out=idle[:], lhsT=zeros[:, 0:P], rhs=zeros[:], start=True, stop=True)

        keep_clock(4)
        spread_g1(0, 0, True)
        spread_w(0, 0, False)
        keep_clock(1)
        spread_g1(0, 1, True)
        quantise_g1(0, 0)
        quantise_w(0, halves[0])
        spread_w(0, 1, False)
        quantise_g1(0, 1)
        quantise_w(0, halves[1])
        load_bias()
        keep_clock(2)
        for k in range(K - 1):
            spread_w(k + 1, 0, True)
            spread_w(k + 1, 1, False)
            for q in range(CHUNKS):
                multiply(0, k, q)
            for q in range(CHUNKS):
                add_bias(0, k, q, q > 0)
            quantise_w(k + 1, slice(0, CHUNKS))
        bank_a = transpose_two(g1_sb[:, 1, 0:2, :], True)
        bank_b = transpose_two(g1_sb[:, 1, 2:4, :], True)
        group_g1(1, 0, bank_a, True)
        group_g1(1, 1, bank_b, True)
        for q in range(CHUNKS):
            multiply(0, K - 1, q)
        for q in range(CHUNKS):
            add_bias(0, K - 1, q, q > 0)
        quantise_g1(1, 0)
        quantise_g1(1, 1)
        transpose_h(0, halves[0:1])
        for q in range(2):
            multiply(1, 0, q)
        transpose_h(0, halves[1:2])
        transpose_h(1, halves)
        for q in range(2, 4):
            multiply(1, 0, q)
        set_gain()
        group_a(0, False)
        group_h(0, 0, True)
        group_h(0, 1, False)
        quantise_a(0)
        for q in range(CHUNKS):
            add_bias(1, 0, q, True)

        for b in range(B - 1):
            more = b + 1 < K
            quantise_h(b)
            group_h(b + 1, 0, True)
            step2(b)
            if b + 1 == GROUP:
                transpose_h(b + 1, halves[1:2])
            if 3 <= b:
                group_h(b + 1, 1, True)
            if more:
                for q in range(CHUNKS - 1):
                    multiply(1, b + 1, q)
                add_bias(1, b + 1, 0, True)
            if 1 <= b:
                mean(b - 1)
                variance(b - 1)
            if more:
                add_bias(1, b + 1, 1, True)
            if 1 <= b:
                inverse_deviation(b - 1)
            if more:
                multiply(1, b + 1, CHUNKS - 1)
                add_bias(1, b + 1, 2, True)
                add_bias(1, b + 1, 3, True)
            if b + 2 < B:
                transpose_h(b + 2, halves[0:1] if b + 2 == GROUP else halves)
                if not more:
                    keep_clock(2)
            if b < 3:
                group_h(b + 1, 1, False)
            if b < 3:
                group_a(b + 1, False)
            if 2 <= b:
                scale_and_shift(b - 2)
            if 1 <= b:
                centre(b - 1)
            if b + 2 == B:
                quantise_h(b + 1)
            residual(b)
            if b < 3:
                quantise_a(b + 1)
        step2(B - 1)
        scale_and_shift(B - 3)
        mean(B - 2)
        variance(B - 2)
        inverse_deviation(B - 2)
        residual(B - 1)
        centre(B - 2)
        mean(B - 1)
        variance(B - 1)
        inverse_deviation(B - 1)
        scale_and_shift(B - 2)
        centre(B - 1)
        scale_and_shift(B - 1)
